import numpy as np
import ml_dtypes


def mxq(x, axis, fmt="e4m3"):
    dtype, down = {"e4m3": (ml_dtypes.float8_e4m3fn, 7), "e5m2": (ml_dtypes.float8_e5m2, 14)}[fmt]
    v = np.moveaxis(np.asarray(x, np.float32).astype(ml_dtypes.bfloat16).astype(np.float64), axis, -1)
    blocks = v.reshape(v.shape[:-1] + (-1, 32))
    amax = np.abs(blocks).max(-1, keepdims=True)
    byte = np.maximum(np.where(amax > 0, np.frexp(amax)[1] - 1 + 127, 0) - down, 1)
    scale = np.exp2(byte - 127.0)
    codes = (blocks / scale).astype(np.float32).astype(dtype).astype(np.float64)
    return np.moveaxis((codes * scale).reshape(v.shape), -1, axis)


WIDE = False


def mx_kscale(k):
    if not WIDE:
        return np.ones(k)
    levels = np.array([10, -10, 5, -5, 0])
    a = np.random.permutation(np.resize(levels, k // 512 * 4)).reshape(k // 512, 4)
    idx = np.arange(k)
    return np.exp2(a[idx // 512, idx % 128 // 32])


BF16 = ml_dtypes.bfloat16


def bf(x):
    return np.asarray(x, np.float32).astype(BF16)


def f64(x):
    return np.asarray(x).astype(np.float64)


E2M1 = np.array([0.0, 0.5, 1.0, 1.5, 2.0, 3.0, 4.0, 6.0, -0.0, -0.5, -1.0, -1.5, -2.0, -3.0, -4.0, -6.0])


def pack_weight(w, fmt):
    k, n = w.shape
    w = f64(bf(w)).reshape(k // 32, 32, n)
    amax = np.abs(w).max(1)
    if fmt == "e4m3":
        byte = np.frexp(amax)[1] - 1 + 127 - 7
    else:
        mant, ex = np.frexp(amax / 6.0)
        byte = np.where(mant > 0.5, ex, ex - 1) + 127
    byte = np.clip(np.where(amax > 0, byte, 1), 1, 254)
    scaled = (w * np.exp2(127.0 - byte)[:, None, :]).reshape(k, n).astype(np.float32)
    by_word = np.ascontiguousarray(scaled.reshape(k // 512, 128, 4, n).transpose(0, 1, 3, 2))
    if fmt == "e4m3":
        words = by_word.astype(ml_dtypes.float8_e4m3fn).view(np.uint8)
    else:
        c = by_word.astype(ml_dtypes.float4_e2m1fn).view(np.uint8) & 0xF
        words = c[..., 0::2] | (c[..., 1::2] << 4)
    return np.ascontiguousarray(words), np.ascontiguousarray(byte.astype(np.uint8).reshape(k // 512, 16, n))


def unpack_weight(words, scales, fmt):
    g, p, n, _ = words.shape
    if fmt == "e4m3":
        vals = np.ascontiguousarray(words).view(ml_dtypes.float8_e4m3fn).astype(np.float64)
    else:
        nib = np.empty((g, p, n, 4), np.uint8)
        nib[..., 0::2] = words & 0xF
        nib[..., 1::2] = words >> 4
        vals = E2M1[nib]
    vals = vals * np.repeat(np.exp2(scales.astype(np.float64) - 127.0), 8, axis=1)[..., None]
    return vals.transpose(0, 1, 3, 2).reshape(g * 512, n)

def pack4(w):
    words, scales = pack_weight(w, "e2m1")
    return words.reshape(words.shape[0], 128, -1), scales


def unpack4(words, scales):
    return unpack_weight(words.reshape(words.shape[0], 128, -1, 2), scales, "e2m1")


B, C, H, W, S = 8, 512, 64, 32, 2
NB = (H // S) * (W // S)


def setup_inputs():
    s = mx_kscale(C)
    x = bf(np.random.standard_normal((B, C, H, W)) * s[None, :, None, None])
    wq = np.random.standard_normal((C, C)) * 1.2 * S / np.sqrt(C) / s[None, :]
    Wq_words, Wq_scales = pack4(np.ascontiguousarray(wq.T))
    bq = bf(np.random.standard_normal(C) * 0.3)
    wk = np.random.standard_normal((C, C)) * 1.2 * S / np.sqrt(C) / s[None, :]
    Wk_words, Wk_scales = pack4(np.ascontiguousarray(wk.T))
    bk = bf(np.random.standard_normal(C) * 0.3)
    return {"x": x,
            "Wq_words": Wq_words, "Wq_scales": Wq_scales,
            "bq": bq,
            "Wk_words": Wk_words, "Wk_scales": Wk_scales,
            "bk": bk}


def reference(x, Wq_words, Wq_scales, bq, Wk_words, Wk_scales, bk):
    x_avg = f64(x).reshape(B, C, H // S, S, W // S, S).mean(axis=(3, 5))
    x_avg = x_avg.reshape(B, C, NB).transpose(0, 2, 1)
    xq = mxq(x_avg, 2, "e4m3")
    Q = (xq @ unpack4(Wq_words, Wq_scales)) + f64(bq)
    K = (xq @ unpack4(Wk_words, Wk_scales)) + f64(bk)
    return Q, K

@@ -1,0 +1,193 @@
+from contextlib import ExitStack
+
+import concourse.masks as masks
+import concourse.mybir as mybir
+
+F32 = mybir.dt.float32
+BF16 = mybir.dt.bfloat16
+U8 = mybir.dt.uint8
+U32 = mybir.dt.uint32
+I32 = mybir.dt.int32
+FP8X4 = mybir.dt.float8_e4m3fn_x4
+FP4X4 = mybir.dt.float4_e2m1fn_x4
+ADD = mybir.AluOpType.add
+ACT = mybir.ActivationFunctionType
+
+P = 128
+PACK = 4
+IMAGES, CHANNELS, HEIGHT, WIDTH = 8, 512, 64, 32
+PIXELS = HEIGHT * WIDTH
+BLOCKS = PIXELS // 4
+OUT = 512
+TILES = BLOCKS // P
+
+FLOPS = 2 * IMAGES * BLOCKS * CHANNELS * 2 * OUT
+
+
+def tile_coarseblockattention_pa_t_kernel(
+    tc, x, Wq_words, Wq_scales, bq, Wk_words, Wk_scales, bk, out_0, out_1
+):
+    nc = tc.nc
+    with ExitStack() as ctx:
+        ctx.enter_context(tc.manual_schedule())
+        consts = ctx.enter_context(tc.tile_pool(name="consts", bufs=1))
+        images = ctx.enter_context(tc.tile_pool(name="images", bufs=3))
+        work = ctx.enter_context(tc.tile_pool(name="work", bufs=2))
+        results = ctx.enter_context(tc.tile_pool(name="results", bufs=3))
+        psum_q = ctx.enter_context(tc.psum_pool(name="psum_q", bufs=3))
+        psum_kt = ctx.enter_context(tc.psum_pool(name="psum_kt", bufs=2))
+        psum_k = ctx.enter_context(tc.psum_pool(name="psum_k", bufs=2))
+
+        def load_image(b):
+            x_sb = images.tile([P, PACK * PIXELS], BF16)
+            nc.sync.dma_start(out=x_sb[:], in_=x[b].rearrange("(p j) h w -> p (j h w)", j=PACK))
+            return x_sb
+
+        x_tiles = [load_image(0), load_image(1)]
+
+        def load_weight(label, words, scales):
+            words_sb = consts.tile([P, 2 * OUT], U8, align_bytes=64, name=label + "_words")
+            plane_sb = consts.tile([P, OUT], U8, align_bytes=64, name=label + "_plane")
+            nc.vector.memset(plane_sb[:].bitcast(I32), 0)
+            nc.sync.dma_start(out=words_sb[:].bitcast(I32), in_=words[0].bitcast(I32))
+            for quadrant in range(4):
+                nc.sync.dma_start(
+                    out=plane_sb[32 * quadrant : 32 * quadrant + 4, :].bitcast(I32),
+                    in_=scales[0, 4 * quadrant : 4 * quadrant + 4, :].bitcast(I32),
+                )
+            return words_sb, plane_sb
+
+        wq_words, wq_plane = load_weight("wq", Wq_words, Wq_scales)
+        wk_words, wk_plane = load_weight("wk", Wk_words, Wk_scales)
+
+        bq_all = consts.tile([P, OUT], BF16)
+        nc.scalar.dma_start(out=bq_all[:], in_=bq.partition_broadcast(P))
+
+        identity = consts.tile([P, P], F32)
+        masks.make_identity(nc, identity[:])
+
+        bk_rows_bf = consts.tile([P, P], BF16)
+        nc.vector.memset(bk_rows_bf[:], 0.0)
+        nc.scalar.dma_start(out=bk_rows_bf[0:TILES, :], in_=bk.rearrange("(o c) -> o c", o=TILES))
+        bk_rows = consts.tile([P, P], F32)
+        nc.vector.tensor_copy(out=bk_rows[:], in_=bk_rows_bf[:])
+        bk_ps = psum_k.tile([P, OUT], F32, name="bk_ps", tag="k_ps")
+        nc.tensor.transpose(bk_ps[:, 0:P], bk_rows[:], identity[:])
+        bk_cols = consts.tile([P, TILES], F32)
+        nc.vector.tensor_copy(out=bk_cols[:], in_=bk_ps[:, 0:TILES])
+
+        def add_rows(x_sb):
+            row_sum = work.tile([P, PACK * PIXELS // 2], F32)
+            rows = x_sb[:].rearrange("p (r i w) -> p r i w", i=2, w=WIDTH)
+            nc.vector.tensor_tensor(
+                out=row_sum[:].rearrange("p (r w) -> p r w", w=WIDTH),
+                in0=rows[:, :, 0, :],
+                in1=rows[:, :, 1, :],
+                op=ADD,
+            )
+            return row_sum
+
+        def add_columns(row_sum):
+            block_sum = work.tile([P, PACK * BLOCKS], F32)
+            columns = row_sum[:].rearrange("p (c e) -> p c e", e=2)
+            nc.vector.tensor_tensor(
+                out=block_sum[:], in0=columns[:, :, 0], in1=columns[:, :, 1], op=ADD
+            )
+            return block_sum
+
+        def round_means(block_sum):
+            x_avg = work.tile([P, BLOCKS, PACK], BF16, align_bytes=64)
+            nc.scalar.activation(
+                out=x_avg[:],
+                in_=block_sum[:].rearrange("p (j n) -> p n j", j=PACK),
+                func=ACT.Copy,
+                scale=0.25,
+            )
+            return x_avg
+
+        def quantise(x_avg):
+            codes = work.tile([P, BLOCKS], U32, align_bytes=64)
+            plane = work.tile([P, BLOCKS], U8, align_bytes=64)
+            nc.vector.quantize_mx(
+                out=codes[:].bitcast(FP8X4),
+                scales=plane[:],
+                in_=x_avg[:].rearrange("p n j -> p (n j)"),
+            )
+            return codes, plane
+
+        def project(codes, plane):
+            kt_banks, q_banks = [], []
+            for g in range(TILES):
+                cols = slice(g * P, (g + 1) * P)
+                kt_ps = psum_kt.tile([P, BLOCKS], F32)
+                nc.tensor.matmul_mx(
+                    out=kt_ps[:],
+                    lhsT=wk_words[:, 2 * g * P : 2 * (g + 1) * P].bitcast(FP4X4),
+                    lhsT_scale=wk_plane[:, cols],
+                    rhs=codes[:].bitcast(FP8X4),
+                    rhs_scale=plane[:],
+                    start=True,
+                    stop=True,
+                )
+                kt_banks.append(kt_ps)
+                q_ps = psum_q.tile([P, OUT], F32)
+                nc.tensor.matmul_mx(
+                    out=q_ps[:],
+                    lhsT=codes[:, cols].bitcast(FP8X4),
+                    lhsT_scale=plane[:, cols],
+                    rhs=wq_words[:].bitcast(FP4X4),
+                    rhs_scale=wq_plane[:],
+                    start=True,
+                    stop=True,
+                )
+                q_banks.append(q_ps)
+            return kt_banks, q_banks
+
+        def bias_kt(kt_banks):
+            kt_sb = work.tile([P, TILES, BLOCKS], F32)
+            for o in range(TILES):
+                nc.scalar.activation(
+                    out=kt_sb[:, o, :],
+                    in_=kt_banks[o][:],
+                    func=ACT.Identity,
+                    bias=bk_cols[:, o : o + 1],
+                )
+            return kt_sb
+
+        def finish_q(b, q_banks):
+            q_out = results.tile([P, TILES, OUT], F32)
+            for t in range(TILES):
+                nc.vector.tensor_tensor(out=q_out[:, t, :], in0=q_banks[t][:], in1=bq_all[:], op=ADD)
+            nc.sync.dma_start(out=out_0[b].rearrange("(t m) o -> m t o", m=P), in_=q_out[:])
+
+        def finish_k(b, kt_sb):
+            k_out = results.tile([P, TILES, OUT], F32)
+            for t in range(TILES):
+                k_ps = psum_k.tile([P, OUT], F32)
+                for o in range(TILES):
+                    nc.tensor.transpose(
+                        k_ps[:, o * P : (o + 1) * P], kt_sb[:, o, t * P : (t + 1) * P], identity[:]
+                    )
+                nc.scalar.copy(out=k_out[:, t, :], in_=k_ps[:])
+            nc.sync.dma_start(out=out_1[b].rearrange("(t m) o -> m t o", m=P), in_=k_out[:])
+
+        x_avg = None
+        for i in range(IMAGES + 1):
+            pooling = i < IMAGES
+            projecting = i > 0
+            if i + 2 < IMAGES:
+                x_tiles.append(load_image(i + 2))
+            if pooling:
+                row_sum = add_rows(x_tiles[i])
+            if projecting:
+                codes, plane = quantise(x_avg)
+                kt_banks, q_banks = project(codes, plane)
+            if pooling:
+                block_sum = add_columns(row_sum)
+            if projecting:
+                kt_sb = bias_kt(kt_banks)
+            if pooling:
+                x_avg = round_means(block_sum)
+            if projecting:
+                finish_q(i - 1, q_banks)
+                finish_k(i - 1, kt_sb)

@@ -17,11 +17,22 @@ P = 128
 PACK = 4
 IMAGES, CHANNELS, HEIGHT, WIDTH = 8, 512, 64, 32
 PIXELS = HEIGHT * WIDTH
-BLOCKS = PIXELS // 4
 OUT = 512
-TILES = BLOCKS // P
+OUT_TILES = OUT // P
+HALVES = 2
+UNITS = IMAGES * HALVES
+UNIT_PIXELS = PIXELS // HALVES
+UNIT_BLOCKS = UNIT_PIXELS // 4
+GROUPS = UNIT_BLOCKS // P
+ROW_BLOCKS = WIDTH // 2
+UNIT_ROWS = UNIT_BLOCKS // ROW_BLOCKS
+TENSOR_ROWS = 2
+TENSOR_BLOCKS = TENSOR_ROWS * ROW_BLOCKS
+VECTOR_ROWS = UNIT_ROWS - TENSOR_ROWS
+VECTOR_BLOCKS = VECTOR_ROWS * ROW_BLOCKS
+IMAGES_AHEAD = 4
 
-FLOPS = 2 * IMAGES * BLOCKS * CHANNELS * 2 * OUT
+FLOPS = 2 * UNITS * UNIT_BLOCKS * CHANNELS * 2 * OUT
 
 
 def tile_coarseblockattention_pa_t_kernel(
@@ -31,19 +42,53 @@ def tile_coarseblockattention_pa_t_kernel(
     with ExitStack() as ctx:
         ctx.enter_context(tc.manual_schedule())
         consts = ctx.enter_context(tc.tile_pool(name="consts", bufs=1))
-        images = ctx.enter_context(tc.tile_pool(name="images", bufs=3))
+        images = ctx.enter_context(tc.tile_pool(name="images", bufs=IMAGES_AHEAD))
         work = ctx.enter_context(tc.tile_pool(name="work", bufs=2))
         results = ctx.enter_context(tc.tile_pool(name="results", bufs=3))
         psum_q = ctx.enter_context(tc.psum_pool(name="psum_q", bufs=3))
         psum_kt = ctx.enter_context(tc.psum_pool(name="psum_kt", bufs=2))
         psum_k = ctx.enter_context(tc.psum_pool(name="psum_k", bufs=2))
+        psum_pool = ctx.enter_context(tc.psum_pool(name="psum_pool", bufs=1))
 
-        def load_image(b):
-            x_sb = images.tile([P, PACK * PIXELS], BF16)
-            nc.sync.dma_start(out=x_sb[:], in_=x[b].rearrange("(p j) h w -> p (j h w)", j=PACK))
+        bq_row = consts.tile([P, OUT], BF16)
+        bk_rows_bf = consts.tile([P, P], BF16)
+        nc.vector.memset(bq_row[:], 0.0)
+        nc.vector.memset(bk_rows_bf[:], 0.0)
+        nc.scalar.dma_start(out=bq_row[0:1, :], in_=bq.rearrange("(o c) -> o c", o=1))
+        nc.scalar.dma_start(
+            out=bk_rows_bf[0:OUT_TILES, :], in_=bk.rearrange("(o c) -> o c", o=OUT_TILES)
+        )
+        ones = consts.tile([P, P], BF16)
+        nc.vector.memset(ones[:], 1.0)
+        identity = consts.tile([P, P], F32)
+        masks.make_identity(nc, identity[:])
+        identity_bf = consts.tile([P, P], BF16)
+        nc.scalar.copy(out=identity_bf[:], in_=identity[:])
+
+        def spread_biases():
+            bq_ps = psum_q.tile([P, OUT], F32, name="bq_ps", tag="q_ps")
+            nc.tensor.matmul(out=bq_ps[:], lhsT=ones[:], rhs=bq_row[:], start=True, stop=True)
+            bq_all = consts.tile([P, OUT], F32)
+            nc.scalar.copy(out=bq_all[:], in_=bq_ps[:])
+            bk_rows = consts.tile([P, P], F32)
+            nc.scalar.copy(out=bk_rows[:], in_=bk_rows_bf[:])
+            bk_ps = psum_k.tile([P, OUT], F32, name="bk_ps", tag="k_ps")
+            nc.tensor.transpose(bk_ps[:, 0:P], bk_rows[:], identity[:])
+            bk_cols = consts.tile([P, OUT_TILES], F32)
+            nc.scalar.copy(out=bk_cols[:], in_=bk_ps[:, 0:OUT_TILES])
+            return bq_all, bk_cols
+
+        bq_all, bk_cols = spread_biases()
+
+        def load_image(b, pieces):
+            x_sb = images.tile([P, PACK, PIXELS], BF16)
+            source = x[b].rearrange("(p j) h w -> p j (h w)", j=PACK)
+            for piece in range(pieces):
+                span = slice(piece * PIXELS // pieces, (piece + 1) * PIXELS // pieces)
+                nc.sync.dma_start(out=x_sb[:, :, span], in_=source[:, :, span])
             return x_sb
 
-        x_tiles = [load_image(0), load_image(1)]
+        x_tiles = [load_image(0, HALVES)]
 
         def load_weight(label, words, scales):
             words_sb = consts.tile([P, 2 * OUT], U8, align_bytes=64, name=label + "_words")
@@ -60,134 +105,151 @@ def tile_coarseblockattention_pa_t_kernel(
         wq_words, wq_plane = load_weight("wq", Wq_words, Wq_scales)
         wk_words, wk_plane = load_weight("wk", Wk_words, Wk_scales)
 
-        bq_all = consts.tile([P, OUT], BF16)
-        nc.scalar.dma_start(out=bq_all[:], in_=bq.partition_broadcast(P))
+        for b in range(1, IMAGES_AHEAD):
+            x_tiles.append(load_image(b, 1))
 
-        identity = consts.tile([P, P], F32)
-        masks.make_identity(nc, identity[:])
+        def unit_pixels(u):
+            half = slice((u % HALVES) * UNIT_PIXELS, (u % HALVES + 1) * UNIT_PIXELS)
+            return x_tiles[u // HALVES][:, :, half].rearrange("p j (r i w) -> p j r i w", i=2, w=WIDTH)
 
-        bk_rows_bf = consts.tile([P, P], BF16)
-        nc.vector.memset(bk_rows_bf[:], 0.0)
-        nc.scalar.dma_start(out=bk_rows_bf[0:TILES, :], in_=bk.rearrange("(o c) -> o c", o=TILES))
-        bk_rows = consts.tile([P, P], F32)
-        nc.vector.tensor_copy(out=bk_rows[:], in_=bk_rows_bf[:])
-        bk_ps = psum_k.tile([P, OUT], F32, name="bk_ps", tag="k_ps")
-        nc.tensor.transpose(bk_ps[:, 0:P], bk_rows[:], identity[:])
-        bk_cols = consts.tile([P, TILES], F32)
-        nc.vector.tensor_copy(out=bk_cols[:], in_=bk_ps[:, 0:TILES])
+        def pool_on_tensor(u):
+            pixels = unit_pixels(u)[:, :, 0:TENSOR_ROWS].rearrange("p j r i (c e) -> p j r i c e", e=2)
+            pool_ps = psum_pool.tile([P, PACK, TENSOR_ROWS, ROW_BLOCKS], F32)
+            for j in range(PACK):
+                for corner in range(4):
+                    nc.tensor.matmul(
+                        out=pool_ps[:, j],
+                        lhsT=identity_bf[:],
+                        rhs=pixels[:, j, :, corner // 2, :, corner % 2],
+                        start=(corner == 0),
+                        stop=(corner == 3),
+                    )
+            return pool_ps
 
-        def add_rows(x_sb):
-            row_sum = work.tile([P, PACK * PIXELS // 2], F32)
-            rows = x_sb[:].rearrange("p (r i w) -> p r i w", i=2, w=WIDTH)
+        def add_rows(u):
+            rows = unit_pixels(u)[:, :, TENSOR_ROWS:UNIT_ROWS]
+            row_sum = work.tile([P, PACK, VECTOR_ROWS, WIDTH], F32)
             nc.vector.tensor_tensor(
-                out=row_sum[:].rearrange("p (r w) -> p r w", w=WIDTH),
-                in0=rows[:, :, 0, :],
-                in1=rows[:, :, 1, :],
-                op=ADD,
+                out=row_sum[:], in0=rows[:, :, :, 0, :], in1=rows[:, :, :, 1, :], op=ADD
             )
             return row_sum
 
         def add_columns(row_sum):
-            block_sum = work.tile([P, PACK * BLOCKS], F32)
-            columns = row_sum[:].rearrange("p (c e) -> p c e", e=2)
+            columns = row_sum[:].rearrange("p j r (c e) -> p (j r c) e", e=2)
+            block_sum = work.tile([P, PACK * VECTOR_BLOCKS], F32)
             nc.vector.tensor_tensor(
                 out=block_sum[:], in0=columns[:, :, 0], in1=columns[:, :, 1], op=ADD
             )
             return block_sum
 
-        def round_means(block_sum):
-            x_avg = work.tile([P, BLOCKS, PACK], BF16, align_bytes=64)
+        def round_means(pool_ps, block_sum):
+            x_avg = work.tile([P, GROUPS, P, PACK], BF16, align_bytes=64)
+            split = TENSOR_BLOCKS // GROUPS
             nc.scalar.activation(
-                out=x_avg[:],
-                in_=block_sum[:].rearrange("p (j n) -> p n j", j=PACK),
+                out=x_avg[:, :, 0:split, :],
+                in_=pool_ps[:].rearrange("p j r c -> p j (r c)").rearrange("p j (m t) -> p t m j", t=GROUPS),
+                func=ACT.Copy,
+                scale=0.25,
+            )
+            nc.scalar.activation(
+                out=x_avg[:, :, split:P, :],
+                in_=block_sum[:].rearrange("p (j m t) -> p t m j", j=PACK, t=GROUPS),
                 func=ACT.Copy,
                 scale=0.25,
             )
             return x_avg
 
         def quantise(x_avg):
-            codes = work.tile([P, BLOCKS], U32, align_bytes=64)
-            plane = work.tile([P, BLOCKS], U8, align_bytes=64)
+            codes = work.tile([P, UNIT_BLOCKS], U32, align_bytes=64)
+            plane = work.tile([P, UNIT_BLOCKS], U8, align_bytes=64)
             nc.vector.quantize_mx(
                 out=codes[:].bitcast(FP8X4),
                 scales=plane[:],
-                in_=x_avg[:].rearrange("p n j -> p (n j)"),
+                in_=x_avg[:].rearrange("p t m j -> p (t m j)"),
             )
             return codes, plane
 
         def project(codes, plane):
-            kt_banks, q_banks = [], []
-            for g in range(TILES):
-                cols = slice(g * P, (g + 1) * P)
-                kt_ps = psum_kt.tile([P, BLOCKS], F32)
-                nc.tensor.matmul_mx(
-                    out=kt_ps[:],
-                    lhsT=wk_words[:, 2 * g * P : 2 * (g + 1) * P].bitcast(FP4X4),
-                    lhsT_scale=wk_plane[:, cols],
-                    rhs=codes[:].bitcast(FP8X4),
-                    rhs_scale=plane[:],
-                    start=True,
-                    stop=True,
-                )
-                kt_banks.append(kt_ps)
+            q_banks = []
+            for t in range(GROUPS):
+                group = slice(t * P, (t + 1) * P)
                 q_ps = psum_q.tile([P, OUT], F32)
                 nc.tensor.matmul_mx(
                     out=q_ps[:],
-                    lhsT=codes[:, cols].bitcast(FP8X4),
-                    lhsT_scale=plane[:, cols],
+                    lhsT=codes[:, group].bitcast(FP8X4),
+                    lhsT_scale=plane[:, group],
                     rhs=wq_words[:].bitcast(FP4X4),
                     rhs_scale=wq_plane[:],
                     start=True,
                     stop=True,
                 )
                 q_banks.append(q_ps)
-            return kt_banks, q_banks
+            kt_banks = []
+            for o in range(OUT_TILES):
+                if o % 2 == 0:
+                    kt_ps = psum_kt.tile([P, 2, UNIT_BLOCKS], F32)
+                    kt_banks.append(kt_ps)
+                nc.tensor.matmul_mx(
+                    out=kt_ps[:, o % 2, :],
+                    lhsT=wk_words[:, 2 * o * P : 2 * (o + 1) * P].bitcast(FP4X4),
+                    lhsT_scale=wk_plane[:, o * P : (o + 1) * P],
+                    rhs=codes[:].bitcast(FP8X4),
+                    rhs_scale=plane[:],
+                    start=True,
+                    stop=True,
+                )
+            return q_banks, kt_banks
 
         def bias_kt(kt_banks):
-            kt_sb = work.tile([P, TILES, BLOCKS], F32)
-            for o in range(TILES):
+            kt_sb = work.tile([P, OUT_TILES, UNIT_BLOCKS], F32)
+            for o in range(OUT_TILES):
                 nc.scalar.activation(
                     out=kt_sb[:, o, :],
-                    in_=kt_banks[o][:],
+                    in_=kt_banks[o // 2][:, o % 2, :],
                     func=ACT.Identity,
                     bias=bk_cols[:, o : o + 1],
                 )
             return kt_sb
 
-        def finish_q(b, q_banks):
-            q_out = results.tile([P, TILES, OUT], F32)
-            for t in range(TILES):
-                nc.vector.tensor_tensor(out=q_out[:, t, :], in0=q_banks[t][:], in1=bq_all[:], op=ADD)
-            nc.sync.dma_start(out=out_0[b].rearrange("(t m) o -> m t o", m=P), in_=q_out[:])
+        def unit_rows(out, u):
+            first = (u % HALVES) * UNIT_BLOCKS
+            rows = out[u // HALVES, first : first + UNIT_BLOCKS, :]
+            return rows.rearrange("(m t) o -> m (t o)", t=GROUPS)
 
-        def finish_k(b, kt_sb):
-            k_out = results.tile([P, TILES, OUT], F32)
-            for t in range(TILES):
+        def finish_q(u, q_banks):
+            q_out = results.tile([P, GROUPS, OUT], F32)
+            for t in range(GROUPS):
+                nc.vector.tensor_tensor(out=q_out[:, t, :], in0=q_banks[t][:], in1=bq_all[:], op=ADD)
+            nc.sync.dma_start(out=unit_rows(out_0, u), in_=q_out[:].rearrange("m t o -> m (t o)"))
+
+        def finish_k(u, kt_sb):
+            k_out = results.tile([P, GROUPS, OUT], F32)
+            for t in range(GROUPS):
                 k_ps = psum_k.tile([P, OUT], F32)
-                for o in range(TILES):
+                for o in range(OUT_TILES):
                     nc.tensor.transpose(
                         k_ps[:, o * P : (o + 1) * P], kt_sb[:, o, t * P : (t + 1) * P], identity[:]
                     )
                 nc.scalar.copy(out=k_out[:, t, :], in_=k_ps[:])
-            nc.sync.dma_start(out=out_1[b].rearrange("(t m) o -> m t o", m=P), in_=k_out[:])
+            nc.sync.dma_start(out=unit_rows(out_1, u), in_=k_out[:].rearrange("m t o -> m (t o)"))
 
         x_avg = None
-        for i in range(IMAGES + 1):
-            pooling = i < IMAGES
-            projecting = i > 0
-            if i + 2 < IMAGES:
-                x_tiles.append(load_image(i + 2))
+        for u in range(UNITS + 1):
+            pooling = u < UNITS
+            projecting = u > 0
             if pooling:
-                row_sum = add_rows(x_tiles[i])
+                pool_ps = pool_on_tensor(u)
+                row_sum = add_rows(u)
             if projecting:
                 codes, plane = quantise(x_avg)
-                kt_banks, q_banks = project(codes, plane)
+                q_banks, kt_banks = project(codes, plane)
             if pooling:
                 block_sum = add_columns(row_sum)
+                x_avg = round_means(pool_ps, block_sum)
             if projecting:
                 kt_sb = bias_kt(kt_banks)
-            if pooling:
-                x_avg = round_means(block_sum)
-            if projecting:
-                finish_q(i - 1, q_banks)
-                finish_k(i - 1, kt_sb)
+                finish_q(u - 1, q_banks)
+                finish_k(u - 1, kt_sb)
+            next_image = u // HALVES + IMAGES_AHEAD
+            if u % HALVES == HALVES - 1 and next_image < IMAGES:
+                x_tiles.append(load_image(next_image, 1))

@@ -26,7 +26,7 @@ UNIT_BLOCKS = UNIT_PIXELS // 4
 GROUPS = UNIT_BLOCKS // P
 ROW_BLOCKS = WIDTH // 2
 UNIT_ROWS = UNIT_BLOCKS // ROW_BLOCKS
-TENSOR_ROWS = 2
+TENSOR_ROWS = 3
 TENSOR_BLOCKS = TENSOR_ROWS * ROW_BLOCKS
 VECTOR_ROWS = UNIT_ROWS - TENSOR_ROWS
 VECTOR_BLOCKS = VECTOR_ROWS * ROW_BLOCKS
@@ -113,14 +113,14 @@ def tile_coarseblockattention_pa_t_kernel(
             return x_tiles[u // HALVES][:, :, half].rearrange("p j (r i w) -> p j r i w", i=2, w=WIDTH)
 
         def pool_on_tensor(u):
-            pixels = unit_pixels(u)[:, :, 0:TENSOR_ROWS].rearrange("p j r i (c e) -> p j r i c e", e=2)
+            pixels = unit_pixels(u).rearrange("p j r i (c e) -> p j r i c e", e=2)
             pool_ps = psum_pool.tile([P, PACK, TENSOR_ROWS, ROW_BLOCKS], F32)
-            for j in range(PACK):
+            for r in range(TENSOR_ROWS):
                 for corner in range(4):
                     nc.tensor.matmul(
-                        out=pool_ps[:, j],
+                        out=pool_ps[:, :, r, :],
                         lhsT=identity_bf[:],
-                        rhs=pixels[:, j, :, corner // 2, :, corner % 2],
+                        rhs=pixels[:, :, r, corner // 2, :, corner % 2],
                         start=(corner == 0),
                         stop=(corner == 3),
                     )
@@ -169,21 +169,7 @@ def tile_coarseblockattention_pa_t_kernel(
             )
             return codes, plane
 
-        def project(codes, plane):
-            q_banks = []
-            for t in range(GROUPS):
-                group = slice(t * P, (t + 1) * P)
-                q_ps = psum_q.tile([P, OUT], F32)
-                nc.tensor.matmul_mx(
-                    out=q_ps[:],
-                    lhsT=codes[:, group].bitcast(FP8X4),
-                    lhsT_scale=plane[:, group],
-                    rhs=wq_words[:].bitcast(FP4X4),
-                    rhs_scale=wq_plane[:],
-                    start=True,
-                    stop=True,
-                )
-                q_banks.append(q_ps)
+        def project_k(codes, plane):
             kt_banks = []
             for o in range(OUT_TILES):
                 if o % 2 == 0:
@@ -198,7 +184,24 @@ def tile_coarseblockattention_pa_t_kernel(
                     start=True,
                     stop=True,
                 )
-            return q_banks, kt_banks
+            return kt_banks
+
+        def project_q(codes, plane):
+            q_banks = []
+            for t in range(GROUPS):
+                group = slice(t * P, (t + 1) * P)
+                q_ps = psum_q.tile([P, OUT], F32)
+                nc.tensor.matmul_mx(
+                    out=q_ps[:],
+                    lhsT=codes[:, group].bitcast(FP8X4),
+                    lhsT_scale=plane[:, group],
+                    rhs=wq_words[:].bitcast(FP4X4),
+                    rhs_scale=wq_plane[:],
+                    start=True,
+                    stop=True,
+                )
+                q_banks.append(q_ps)
+            return q_banks
 
         def bias_kt(kt_banks):
             kt_sb = work.tile([P, OUT_TILES, UNIT_BLOCKS], F32)
@@ -211,6 +214,17 @@ def tile_coarseblockattention_pa_t_kernel(
                 )
             return kt_sb
 
+        def transpose_k(kt_sb):
+            k_banks = []
+            for t in range(GROUPS):
+                k_ps = psum_k.tile([P, OUT], F32)
+                for o in range(OUT_TILES):
+                    nc.tensor.transpose(
+                        k_ps[:, o * P : (o + 1) * P], kt_sb[:, o, t * P : (t + 1) * P], identity[:]
+                    )
+                k_banks.append(k_ps)
+            return k_banks
+
         def unit_rows(out, u):
             first = (u % HALVES) * UNIT_BLOCKS
             rows = out[u // HALVES, first : first + UNIT_BLOCKS, :]
@@ -222,34 +236,38 @@ def tile_coarseblockattention_pa_t_kernel(
                 nc.vector.tensor_tensor(out=q_out[:, t, :], in0=q_banks[t][:], in1=bq_all[:], op=ADD)
             nc.sync.dma_start(out=unit_rows(out_0, u), in_=q_out[:].rearrange("m t o -> m (t o)"))
 
-        def finish_k(u, kt_sb):
+        def finish_k(u, k_banks):
             k_out = results.tile([P, GROUPS, OUT], F32)
             for t in range(GROUPS):
-                k_ps = psum_k.tile([P, OUT], F32)
-                for o in range(OUT_TILES):
-                    nc.tensor.transpose(
-                        k_ps[:, o * P : (o + 1) * P], kt_sb[:, o, t * P : (t + 1) * P], identity[:]
-                    )
-                nc.scalar.copy(out=k_out[:, t, :], in_=k_ps[:])
+                nc.scalar.copy(out=k_out[:, t, :], in_=k_banks[t][:])
             nc.sync.dma_start(out=unit_rows(out_1, u), in_=k_out[:].rearrange("m t o -> m (t o)"))
 
-        x_avg = None
-        for u in range(UNITS + 1):
-            pooling = u < UNITS
-            projecting = u > 0
+        pool_ps = pool_on_tensor(0)
+        x_avg, q_banks, kt_sb = None, None, None
+        for step in range(UNITS + 2):
+            pooling = step < UNITS
+            projecting = 1 <= step <= UNITS
+            finishing = step >= 2
             if pooling:
-                pool_ps = pool_on_tensor(u)
-                row_sum = add_rows(u)
+                row_sum = add_rows(step)
             if projecting:
                 codes, plane = quantise(x_avg)
-                q_banks, kt_banks = project(codes, plane)
+                kt_banks = project_k(codes, plane)
+            if finishing:
+                k_banks = transpose_k(kt_sb)
+                q_banks_to_finish = q_banks
+            if projecting:
+                q_banks = project_q(codes, plane)
             if pooling:
                 block_sum = add_columns(row_sum)
                 x_avg = round_means(pool_ps, block_sum)
+            if step + 1 < UNITS:
+                pool_ps = pool_on_tensor(step + 1)
+            if finishing:
+                finish_q(step - 2, q_banks_to_finish)
+                finish_k(step - 2, k_banks)
             if projecting:
                 kt_sb = bias_kt(kt_banks)
-                finish_q(u - 1, q_banks)
-                finish_k(u - 1, kt_sb)
-            next_image = u // HALVES + IMAGES_AHEAD
-            if u % HALVES == HALVES - 1 and next_image < IMAGES:
+            next_image = step // HALVES + IMAGES_AHEAD
+            if step % HALVES == HALVES - 1 and next_image < IMAGES:
                 x_tiles.append(load_image(next_image, 1))

@@ -54,8 +54,8 @@ def tile_coarseblockattention_pa_t_kernel(
         bk_rows_bf = consts.tile([P, P], BF16)
         nc.vector.memset(bq_row[:], 0.0)
         nc.vector.memset(bk_rows_bf[:], 0.0)
-        nc.scalar.dma_start(out=bq_row[0:1, :], in_=bq.rearrange("(o c) -> o c", o=1))
-        nc.scalar.dma_start(
+        nc.sync.dma_start(out=bq_row[0:1, :], in_=bq.rearrange("(o c) -> o c", o=1))
+        nc.sync.dma_start(
             out=bk_rows_bf[0:OUT_TILES, :], in_=bk.rearrange("(o c) -> o c", o=OUT_TILES)
         )
         ones = consts.tile([P, P], BF16)
@@ -263,11 +263,11 @@ def tile_coarseblockattention_pa_t_kernel(
                 x_avg = round_means(pool_ps, block_sum)
             if step + 1 < UNITS:
                 pool_ps = pool_on_tensor(step + 1)
+            if projecting:
+                kt_sb = bias_kt(kt_banks)
             if finishing:
                 finish_q(step - 2, q_banks_to_finish)
                 finish_k(step - 2, k_banks)
-            if projecting:
-                kt_sb = bias_kt(kt_banks)
             next_image = step // HALVES + IMAGES_AHEAD
             if step % HALVES == HALVES - 1 and next_image < IMAGES:
                 x_tiles.append(load_image(next_image, 1))

@@ -30,6 +30,7 @@ TENSOR_ROWS = 3
 TENSOR_BLOCKS = TENSOR_ROWS * ROW_BLOCKS
 VECTOR_ROWS = UNIT_ROWS - TENSOR_ROWS
 VECTOR_BLOCKS = VECTOR_ROWS * ROW_BLOCKS
+RUN = 4
 IMAGES_AHEAD = 4
 
 FLOPS = 2 * UNITS * UNIT_BLOCKS * CHANNELS * 2 * OUT
@@ -50,6 +51,19 @@ def tile_coarseblockattention_pa_t_kernel(
         psum_k = ctx.enter_context(tc.psum_pool(name="psum_k", bufs=2))
         psum_pool = ctx.enter_context(tc.psum_pool(name="psum_pool", bufs=1))
 
+        def load_pixels(x_sb, b, pixels):
+            source = x[b].rearrange("(p j) h w -> p j (h w)", j=PACK)
+            nc.sync.dma_start(out=x_sb[:, :, pixels], in_=source[:, :, pixels])
+
+        def load_image(b):
+            x_sb = images.tile([P, PACK, PIXELS], BF16)
+            load_pixels(x_sb, b, slice(0, PIXELS))
+            return x_sb
+
+        x_first = images.tile([P, PACK, PIXELS], BF16, name="x_first", tag="x_sb")
+        load_pixels(x_first, 0, slice(0, UNIT_PIXELS))
+        x_tiles = [x_first]
+
         bq_row = consts.tile([P, OUT], BF16)
         bk_rows_bf = consts.tile([P, P], BF16)
         nc.vector.memset(bq_row[:], 0.0)
@@ -58,6 +72,7 @@ def tile_coarseblockattention_pa_t_kernel(
         nc.sync.dma_start(
             out=bk_rows_bf[0:OUT_TILES, :], in_=bk.rearrange("(o c) -> o c", o=OUT_TILES)
         )
+        load_pixels(x_first, 0, slice(UNIT_PIXELS, PIXELS))
         ones = consts.tile([P, P], BF16)
         nc.vector.memset(ones[:], 1.0)
         identity = consts.tile([P, P], F32)
@@ -78,18 +93,6 @@ def tile_coarseblockattention_pa_t_kernel(
             nc.scalar.copy(out=bk_cols[:], in_=bk_ps[:, 0:OUT_TILES])
             return bq_all, bk_cols
 
-        bq_all, bk_cols = spread_biases()
-
-        def load_image(b, pieces):
-            x_sb = images.tile([P, PACK, PIXELS], BF16)
-            source = x[b].rearrange("(p j) h w -> p j (h w)", j=PACK)
-            for piece in range(pieces):
-                span = slice(piece * PIXELS // pieces, (piece + 1) * PIXELS // pieces)
-                nc.sync.dma_start(out=x_sb[:, :, span], in_=source[:, :, span])
-            return x_sb
-
-        x_tiles = [load_image(0, HALVES)]
-
         def load_weight(label, words, scales):
             words_sb = consts.tile([P, 2 * OUT], U8, align_bytes=64, name=label + "_words")
             plane_sb = consts.tile([P, OUT], U8, align_bytes=64, name=label + "_plane")
@@ -106,7 +109,7 @@ def tile_coarseblockattention_pa_t_kernel(
         wk_words, wk_plane = load_weight("wk", Wk_words, Wk_scales)
 
         for b in range(1, IMAGES_AHEAD):
-            x_tiles.append(load_image(b, 1))
+            x_tiles.append(load_image(b))
 
         def unit_pixels(u):
             half = slice((u % HALVES) * UNIT_PIXELS, (u % HALVES + 1) * UNIT_PIXELS)
@@ -143,17 +146,18 @@ def tile_coarseblockattention_pa_t_kernel(
             return block_sum
 
         def round_means(pool_ps, block_sum):
-            x_avg = work.tile([P, GROUPS, P, PACK], BF16, align_bytes=64)
-            split = TENSOR_BLOCKS // GROUPS
+            x_avg = work.tile([P, UNIT_BLOCKS, PACK], BF16, align_bytes=64)
+            words = x_avg[:].rearrange("p (c i) j -> p c j i", i=RUN)
+            split = TENSOR_BLOCKS // RUN
             nc.scalar.activation(
-                out=x_avg[:, :, 0:split, :],
-                in_=pool_ps[:].rearrange("p j r c -> p j (r c)").rearrange("p j (m t) -> p t m j", t=GROUPS),
+                out=words[:, split : UNIT_BLOCKS // RUN],
+                in_=block_sum[:].rearrange("p (j c i) -> p c j i", j=PACK, i=RUN),
                 func=ACT.Copy,
                 scale=0.25,
             )
             nc.scalar.activation(
-                out=x_avg[:, :, split:P, :],
-                in_=block_sum[:].rearrange("p (j m t) -> p t m j", j=PACK, t=GROUPS),
+                out=words[:, 0:split],
+                in_=pool_ps[:].rearrange("p j r c -> p j (r c)").rearrange("p j (c i) -> p c j i", i=RUN),
                 func=ACT.Copy,
                 scale=0.25,
             )
@@ -165,7 +169,7 @@ def tile_coarseblockattention_pa_t_kernel(
             nc.vector.quantize_mx(
                 out=codes[:].bitcast(FP8X4),
                 scales=plane[:],
-                in_=x_avg[:].rearrange("p t m j -> p (t m j)"),
+                in_=x_avg[:].rearrange("p n j -> p (n j)"),
             )
             return codes, plane
 
@@ -228,21 +232,22 @@ def tile_coarseblockattention_pa_t_kernel(
         def unit_rows(out, u):
             first = (u % HALVES) * UNIT_BLOCKS
             rows = out[u // HALVES, first : first + UNIT_BLOCKS, :]
-            return rows.rearrange("(m t) o -> m (t o)", t=GROUPS)
+            return rows.rearrange("(t m) o -> m t o", t=GROUPS)
 
         def finish_q(u, q_banks):
             q_out = results.tile([P, GROUPS, OUT], F32)
             for t in range(GROUPS):
                 nc.vector.tensor_tensor(out=q_out[:, t, :], in0=q_banks[t][:], in1=bq_all[:], op=ADD)
-            nc.sync.dma_start(out=unit_rows(out_0, u), in_=q_out[:].rearrange("m t o -> m (t o)"))
+            nc.sync.dma_start(out=unit_rows(out_0, u), in_=q_out[:])
 
         def finish_k(u, k_banks):
             k_out = results.tile([P, GROUPS, OUT], F32)
             for t in range(GROUPS):
                 nc.scalar.copy(out=k_out[:, t, :], in_=k_banks[t][:])
-            nc.sync.dma_start(out=unit_rows(out_1, u), in_=k_out[:].rearrange("m t o -> m (t o)"))
+            nc.sync.dma_start(out=unit_rows(out_1, u), in_=k_out[:])
 
         pool_ps = pool_on_tensor(0)
+        bq_all, bk_cols = spread_biases()
         x_avg, q_banks, kt_sb = None, None, None
         for step in range(UNITS + 2):
             pooling = step < UNITS
@@ -270,4 +275,4 @@ def tile_coarseblockattention_pa_t_kernel(
                 finish_k(step - 2, k_banks)
             next_image = step // HALVES + IMAGES_AHEAD
             if step % HALVES == HALVES - 1 and next_image < IMAGES:
-                x_tiles.append(load_image(next_image, 1))
+                x_tiles.append(load_image(next_image))

@@ -11,12 +11,14 @@ I32 = mybir.dt.int32
 FP8X4 = mybir.dt.float8_e4m3fn_x4
 FP4X4 = mybir.dt.float4_e2m1fn_x4
 ADD = mybir.AluOpType.add
+MULT = mybir.AluOpType.mult
 ACT = mybir.ActivationFunctionType
 
 P = 128
 PACK = 4
 IMAGES, CHANNELS, HEIGHT, WIDTH = 8, 512, 64, 32
 PIXELS = HEIGHT * WIDTH
+BLOCK_PIXELS = 4
 OUT = 512
 OUT_TILES = OUT // P
 HALVES = 2
@@ -138,30 +140,22 @@ def tile_coarseblockattention_pa_t_kernel(
             return row_sum
 
         def add_columns(row_sum):
-            columns = row_sum[:].rearrange("p j r (c e) -> p (j r c) e", e=2)
-            block_sum = work.tile([P, PACK * VECTOR_BLOCKS], F32)
+            columns = row_sum[:].rearrange("p j r (c e) -> p (r c) j e", e=2)
+            x_sum = work.tile([P, UNIT_BLOCKS, PACK], BF16, align_bytes=64)
             nc.vector.tensor_tensor(
-                out=block_sum[:], in0=columns[:, :, 0], in1=columns[:, :, 1], op=ADD
+                out=x_sum[:, TENSOR_BLOCKS:UNIT_BLOCKS, :],
+                in0=columns[:, :, :, 0],
+                in1=columns[:, :, :, 1],
+                op=ADD,
             )
-            return block_sum
+            return x_sum
 
-        def round_means(pool_ps, block_sum):
-            x_avg = work.tile([P, UNIT_BLOCKS, PACK], BF16, align_bytes=64)
-            words = x_avg[:].rearrange("p (c i) j -> p c j i", i=RUN)
-            split = TENSOR_BLOCKS // RUN
-            nc.scalar.activation(
-                out=words[:, split : UNIT_BLOCKS // RUN],
-                in_=block_sum[:].rearrange("p (j c i) -> p c j i", j=PACK, i=RUN),
-                func=ACT.Copy,
-                scale=0.25,
-            )
-            nc.scalar.activation(
-                out=words[:, 0:split],
+        def round_tensor_sums(pool_ps, x_sum):
+            words = x_sum[:].rearrange("p (c i) j -> p c j i", i=RUN)
+            nc.scalar.copy(
+                out=words[:, 0 : TENSOR_BLOCKS // RUN],
                 in_=pool_ps[:].rearrange("p j r c -> p j (r c)").rearrange("p j (c i) -> p c j i", i=RUN),
-                func=ACT.Copy,
-                scale=0.25,
             )
-            return x_avg
 
         def quantise(x_avg):
             codes = work.tile([P, UNIT_BLOCKS], U32, align_bytes=64)
@@ -214,6 +208,7 @@ def tile_coarseblockattention_pa_t_kernel(
                     out=kt_sb[:, o, :],
                     in_=kt_banks[o // 2][:, o % 2, :],
                     func=ACT.Identity,
+                    scale=1.0 / BLOCK_PIXELS,
                     bias=bk_cols[:, o : o + 1],
                 )
             return kt_sb
@@ -237,7 +232,14 @@ def tile_coarseblockattention_pa_t_kernel(
         def finish_q(u, q_banks):
             q_out = results.tile([P, GROUPS, OUT], F32)
             for t in range(GROUPS):
-                nc.vector.tensor_tensor(out=q_out[:, t, :], in0=q_banks[t][:], in1=bq_all[:], op=ADD)
+                nc.vector.scalar_tensor_tensor(
+                    out=q_out[:, t, :],
+                    in0=q_banks[t][:],
+                    scalar=1.0 / BLOCK_PIXELS,
+                    in1=bq_all[:],
+                    op0=MULT,
+                    op1=ADD,
+                )
             nc.sync.dma_start(out=unit_rows(out_0, u), in_=q_out[:])
 
         def finish_k(u, k_banks):
@@ -264,8 +266,8 @@ def tile_coarseblockattention_pa_t_kernel(
             if projecting:
                 q_banks = project_q(codes, plane)
             if pooling:
-                block_sum = add_columns(row_sum)
-                x_avg = round_means(pool_ps, block_sum)
+                x_avg = add_columns(row_sum)
+                round_tensor_sums(pool_ps, x_avg)
             if step + 1 < UNITS:
                 pool_ps = pool_on_tensor(step + 1)
             if projecting:

@@ -33,6 +33,7 @@ TENSOR_BLOCKS = TENSOR_ROWS * ROW_BLOCKS
 VECTOR_ROWS = UNIT_ROWS - TENSOR_ROWS
 VECTOR_BLOCKS = VECTOR_ROWS * ROW_BLOCKS
 RUN = 4
+PAIR = 2
 IMAGES_AHEAD = 4
 
 FLOPS = 2 * UNITS * UNIT_BLOCKS * CHANNELS * 2 * OUT
@@ -140,13 +141,11 @@ def tile_coarseblockattention_pa_t_kernel(
             return row_sum
 
         def add_columns(row_sum):
-            columns = row_sum[:].rearrange("p j r (c e) -> p (r c) j e", e=2)
+            columns = row_sum[:].rearrange("p j r (c i e) -> p (r c) j i e", i=PAIR, e=2)
             x_sum = work.tile([P, UNIT_BLOCKS, PACK], BF16, align_bytes=64)
+            words = x_sum[:, TENSOR_BLOCKS:UNIT_BLOCKS, :].rearrange("p (c i) j -> p c j i", i=PAIR)
             nc.vector.tensor_tensor(
-                out=x_sum[:, TENSOR_BLOCKS:UNIT_BLOCKS, :],
-                in0=columns[:, :, :, 0],
-                in1=columns[:, :, :, 1],
-                op=ADD,
+                out=words, in0=columns[:, :, :, :, 0], in1=columns[:, :, :, :, 1], op=ADD
             )
             return x_sum
 

@@ -21,61 +21,75 @@ PIXELS = HEIGHT * WIDTH
 BLOCK_PIXELS = 4
 OUT = 512
 OUT_TILES = OUT // P
-HALVES = 2
-UNITS = IMAGES * HALVES
-UNIT_PIXELS = PIXELS // HALVES
-UNIT_BLOCKS = UNIT_PIXELS // 4
-GROUPS = UNIT_BLOCKS // P
 ROW_BLOCKS = WIDTH // 2
-UNIT_ROWS = UNIT_BLOCKS // ROW_BLOCKS
-TENSOR_ROWS = 3
-TENSOR_BLOCKS = TENSOR_ROWS * ROW_BLOCKS
-VECTOR_ROWS = UNIT_ROWS - TENSOR_ROWS
-VECTOR_BLOCKS = VECTOR_ROWS * ROW_BLOCKS
+GROUP_ROWS = P // ROW_BLOCKS
+GROUP_PIXELS = P * BLOCK_PIXELS
+IMAGE_GROUPS = PIXELS // GROUP_PIXELS
+BANK = 512
+STEADY = (((0, 0, 256), (0, 256, 128)), ((0, 3), (1, 0), (1, 1), (1, 2), (1, 3)), False)
+MIDDLE = (((0, 0, 512),), ((1, 0), (1, 1), (1, 2), (1, 3)), False)
+DRAIN = (((0, 0, 512), (1, 0, 256)), ((1, 2), (1, 3)), True)
+LAYOUT = [[(2, STEADY), (2, STEADY)]] + [[(4, STEADY)]] * 5 + [[(2, MIDDLE), (2, MIDDLE)]] + [[(2, DRAIN), (2, DRAIN)]]
 RUN = 4
 PAIR = 2
-IMAGES_AHEAD = 4
+IMAGES_AHEAD = 5
 
-FLOPS = 2 * UNITS * UNIT_BLOCKS * CHANNELS * 2 * OUT
+FLOPS = 2 * IMAGES * IMAGE_GROUPS * P * CHANNELS * 2 * OUT
 
 
 def tile_coarseblockattention_pa_t_kernel(
     tc, x, Wq_words, Wq_scales, bq, Wk_words, Wk_scales, bk, out_0, out_1
 ):
     nc = tc.nc
+    units = []
+    for b in range(IMAGES):
+        first = 0
+        for groups, plan in LAYOUT[b]:
+            units.append((b, first, groups, plan))
+            first += groups
+    pieces = [[1, 1, 2], [2, 2]] + [[IMAGE_GROUPS]] * (IMAGES - 2)
+
     with ExitStack() as ctx:
         ctx.enter_context(tc.manual_schedule())
         consts = ctx.enter_context(tc.tile_pool(name="consts", bufs=1))
         images = ctx.enter_context(tc.tile_pool(name="images", bufs=IMAGES_AHEAD))
         work = ctx.enter_context(tc.tile_pool(name="work", bufs=2))
-        results = ctx.enter_context(tc.tile_pool(name="results", bufs=3))
-        psum_q = ctx.enter_context(tc.psum_pool(name="psum_q", bufs=3))
-        psum_kt = ctx.enter_context(tc.psum_pool(name="psum_kt", bufs=2))
-        psum_k = ctx.enter_context(tc.psum_pool(name="psum_k", bufs=2))
+        turned_pool = ctx.enter_context(tc.tile_pool(name="turned_pool", bufs=3))
+        results = ctx.enter_context(tc.tile_pool(name="results", bufs=4))
+        psum_direct = ctx.enter_context(tc.psum_pool(name="psum_direct", bufs=3))
+        psum_turned = ctx.enter_context(tc.psum_pool(name="psum_turned", bufs=2))
+        psum_back = ctx.enter_context(tc.psum_pool(name="psum_back", bufs=2))
         psum_pool = ctx.enter_context(tc.psum_pool(name="psum_pool", bufs=1))
 
-        def load_pixels(x_sb, b, pixels):
+        def load_piece(x_sb, b, first, groups):
             source = x[b].rearrange("(p j) h w -> p j (h w)", j=PACK)
+            pixels = slice(first * GROUP_PIXELS, (first + groups) * GROUP_PIXELS)
             nc.sync.dma_start(out=x_sb[:, :, pixels], in_=source[:, :, pixels])
 
-        def load_image(b):
-            x_sb = images.tile([P, PACK, PIXELS], BF16)
-            load_pixels(x_sb, b, slice(0, PIXELS))
-            return x_sb
+        def load_image(b, first_piece=0):
+            if first_piece == 0:
+                x_sb = images.tile([P, PACK, PIXELS], BF16)
+                x_tiles.append(x_sb)
+            for i in range(first_piece, len(pieces[b])):
+                load_piece(x_tiles[b], b, sum(pieces[b][0:i]), pieces[b][i])
 
+        x_tiles = []
         x_first = images.tile([P, PACK, PIXELS], BF16, name="x_first", tag="x_sb")
-        load_pixels(x_first, 0, slice(0, UNIT_PIXELS))
-        x_tiles = [x_first]
+        x_tiles.append(x_first)
+        load_piece(x_first, 0, 0, pieces[0][0])
+        load_piece(x_first, 0, pieces[0][0], pieces[0][1])
 
-        bq_row = consts.tile([P, OUT], BF16)
-        bk_rows_bf = consts.tile([P, P], BF16)
-        nc.vector.memset(bq_row[:], 0.0)
-        nc.vector.memset(bk_rows_bf[:], 0.0)
-        nc.sync.dma_start(out=bq_row[0:1, :], in_=bq.rearrange("(o c) -> o c", o=1))
-        nc.sync.dma_start(
-            out=bk_rows_bf[0:OUT_TILES, :], in_=bk.rearrange("(o c) -> o c", o=OUT_TILES)
-        )
-        load_pixels(x_first, 0, slice(UNIT_PIXELS, PIXELS))
+        bias_row = consts.tile([P, 2, OUT], BF16)
+        bias_rows_bf = consts.tile([P, P], BF16)
+        nc.vector.memset(bias_row[:], 0.0)
+        nc.vector.memset(bias_rows_bf[:], 0.0)
+        for which, bias in enumerate((bq, bk)):
+            nc.sync.dma_start(out=bias_row[0:1, which, :], in_=bias.rearrange("(o c) -> o c", o=1))
+            nc.sync.dma_start(
+                out=bias_rows_bf[which * OUT_TILES : (which + 1) * OUT_TILES, :],
+                in_=bias.rearrange("(o c) -> o c", o=OUT_TILES),
+            )
+        load_image(0, first_piece=2)
         ones = consts.tile([P, P], BF16)
         nc.vector.memset(ones[:], 1.0)
         identity = consts.tile([P, P], F32)
@@ -84,17 +98,33 @@ def tile_coarseblockattention_pa_t_kernel(
         nc.scalar.copy(out=identity_bf[:], in_=identity[:])
 
         def spread_biases():
-            bq_ps = psum_q.tile([P, OUT], F32, name="bq_ps", tag="q_ps")
-            nc.tensor.matmul(out=bq_ps[:], lhsT=ones[:], rhs=bq_row[:], start=True, stop=True)
-            bq_all = consts.tile([P, OUT], F32)
-            nc.scalar.copy(out=bq_all[:], in_=bq_ps[:])
-            bk_rows = consts.tile([P, P], F32)
-            nc.scalar.copy(out=bk_rows[:], in_=bk_rows_bf[:])
-            bk_ps = psum_k.tile([P, OUT], F32, name="bk_ps", tag="k_ps")
-            nc.tensor.transpose(bk_ps[:, 0:P], bk_rows[:], identity[:])
-            bk_cols = consts.tile([P, OUT_TILES], F32)
-            nc.scalar.copy(out=bk_cols[:], in_=bk_ps[:, 0:OUT_TILES])
-            return bq_all, bk_cols
+            spread = {}
+            for which in range(2):
+                widest = max(first + width for plan in (STEADY, MIDDLE, DRAIN) for w, first, width in plan[0] if w == which)
+                bias_ps = psum_direct.tile([P, BANK], F32, name="bias_ps", tag="direct_ps")
+                nc.tensor.matmul(
+                    out=bias_ps[:, 0:widest],
+                    lhsT=ones[:],
+                    rhs=bias_row[:, which, 0:widest],
+                    start=True,
+                    stop=True,
+                )
+                for plan in (STEADY, MIDDLE, DRAIN):
+                    for w, first, width in plan[0]:
+                        if w == which and (w, first, width) not in spread:
+                            bias_all = consts.tile(
+                                [P, BANK // width, width], F32, name="bias_all_%d_%d_%d" % (w, first, width)
+                            )
+                            for t in range(BANK // width):
+                                nc.scalar.copy(out=bias_all[:, t, :], in_=bias_ps[:, first : first + width])
+                            spread[(w, first, width)] = bias_all
+            bias_rows = consts.tile([P, P], F32)
+            nc.scalar.copy(out=bias_rows[:], in_=bias_rows_bf[:])
+            cols_ps = psum_back.tile([P, BANK], F32, name="cols_ps", tag="back_ps")
+            nc.tensor.transpose(cols_ps[:, 0:P], bias_rows[:], identity[:])
+            bias_cols = consts.tile([P, 2 * OUT_TILES], F32)
+            nc.scalar.copy(out=bias_cols[:], in_=cols_ps[:, 0 : 2 * OUT_TILES])
+            return spread, bias_cols
 
         def load_weight(label, words, scales):
             words_sb = consts.tile([P, 2 * OUT], U8, align_bytes=64, name=label + "_words")
@@ -108,172 +138,213 @@ def tile_coarseblockattention_pa_t_kernel(
                 )
             return words_sb, plane_sb
 
-        wq_words, wq_plane = load_weight("wq", Wq_words, Wq_scales)
-        wk_words, wk_plane = load_weight("wk", Wk_words, Wk_scales)
+        weights = [load_weight("wq", Wq_words, Wq_scales), load_weight("wk", Wk_words, Wk_scales)]
 
         for b in range(1, IMAGES_AHEAD):
-            x_tiles.append(load_image(b))
+            load_image(b)
 
-        def unit_pixels(u):
-            half = slice((u % HALVES) * UNIT_PIXELS, (u % HALVES + 1) * UNIT_PIXELS)
-            return x_tiles[u // HALVES][:, :, half].rearrange("p j (r i w) -> p j r i w", i=2, w=WIDTH)
+        def tensor_rows(unit):
+            return 3 * unit[2] // 2
 
-        def pool_on_tensor(u):
-            pixels = unit_pixels(u).rearrange("p j r i (c e) -> p j r i c e", e=2)
-            pool_ps = psum_pool.tile([P, PACK, TENSOR_ROWS, ROW_BLOCKS], F32)
-            for r in range(TENSOR_ROWS):
-                for corner in range(4):
-                    nc.tensor.matmul(
-                        out=pool_ps[:, :, r, :],
-                        lhsT=identity_bf[:],
-                        rhs=pixels[:, :, r, corner // 2, :, corner % 2],
-                        start=(corner == 0),
-                        stop=(corner == 3),
-                    )
+        def unit_pixels(unit):
+            b, first, groups = unit[0:3]
+            pixels = slice(first * GROUP_PIXELS, (first + groups) * GROUP_PIXELS)
+            return x_tiles[b][:, :, pixels].rearrange("p j (r i w) -> p j r i w", i=2, w=WIDTH)
+
+        def pool_corner(unit, pool_ps, corner):
+            rows = tensor_rows(unit)
+            pixels = unit_pixels(unit).rearrange("p j r i (c e) -> p j r i c e", e=2)
+            nc.tensor.matmul(
+                out=pool_ps[:, :, 0:rows, :],
+                lhsT=identity_bf[:],
+                rhs=pixels[:, :, 0:rows, corner // 2, :, corner % 2],
+                start=(corner == 0),
+                stop=(corner == BLOCK_PIXELS - 1),
+            )
+
+        def new_pool_ps(unit):
+            pool_ps = psum_pool.tile([P, PACK, tensor_rows(unit), ROW_BLOCKS], F32)
             return pool_ps
 
-        def add_rows(u):
-            rows = unit_pixels(u)[:, :, TENSOR_ROWS:UNIT_ROWS]
-            row_sum = work.tile([P, PACK, VECTOR_ROWS, WIDTH], F32)
-            nc.vector.tensor_tensor(
-                out=row_sum[:], in0=rows[:, :, :, 0, :], in1=rows[:, :, :, 1, :], op=ADD
-            )
+        def add_rows(unit):
+            b, first, groups = unit[0:3]
+            skipped = tensor_rows(unit)
+            rows = unit_pixels(unit)
+            row_sum = work.tile([P, PACK, groups * GROUP_ROWS - skipped, WIDTH], F32)
+            piece_first = 0
+            for piece in pieces[b]:
+                low, high = max(piece_first, first), min(piece_first + piece, first + groups)
+                if low < high:
+                    r0 = max((low - first) * GROUP_ROWS, skipped)
+                    r1 = (high - first) * GROUP_ROWS
+                    nc.vector.tensor_tensor(
+                        out=row_sum[:, :, r0 - skipped : r1 - skipped, :],
+                        in0=rows[:, :, r0:r1, 0, :],
+                        in1=rows[:, :, r0:r1, 1, :],
+                        op=ADD,
+                    )
+                piece_first += piece
             return row_sum
 
-        def add_columns(row_sum):
-            columns = row_sum[:].rearrange("p j r (c i e) -> p (r c) j i e", i=PAIR, e=2)
-            x_sum = work.tile([P, UNIT_BLOCKS, PACK], BF16, align_bytes=64)
-            words = x_sum[:, TENSOR_BLOCKS:UNIT_BLOCKS, :].rearrange("p (c i) j -> p c j i", i=PAIR)
-            nc.vector.tensor_tensor(
-                out=words, in0=columns[:, :, :, :, 0], in1=columns[:, :, :, :, 1], op=ADD
+        def round_tensor_sums(unit, pool_ps):
+            x_sum = work.tile([P, unit[2] * P, PACK], BF16, align_bytes=64)
+            words = x_sum[:].rearrange("p (c i) j -> p c j i", i=RUN)
+            nc.scalar.copy(
+                out=words[:, 0 : tensor_rows(unit) * ROW_BLOCKS // RUN],
+                in_=pool_ps[:].rearrange("p j r c -> p j (r c)").rearrange("p j (c i) -> p c j i", i=RUN),
             )
             return x_sum
 
-        def round_tensor_sums(pool_ps, x_sum):
-            words = x_sum[:].rearrange("p (c i) j -> p c j i", i=RUN)
-            nc.scalar.copy(
-                out=words[:, 0 : TENSOR_BLOCKS // RUN],
-                in_=pool_ps[:].rearrange("p j r c -> p j (r c)").rearrange("p j (c i) -> p c j i", i=RUN),
+        def add_columns(unit, row_sum, x_sum):
+            columns = row_sum[:].rearrange("p j r (c i e) -> p (r c) j i e", i=PAIR, e=2)
+            words = x_sum[:, tensor_rows(unit) * ROW_BLOCKS : unit[2] * P, :].rearrange(
+                "p (c i) j -> p c j i", i=PAIR
+            )
+            nc.vector.tensor_tensor(
+                out=words, in0=columns[:, :, :, :, 0], in1=columns[:, :, :, :, 1], op=ADD
             )
 
-        def quantise(x_avg):
-            codes = work.tile([P, UNIT_BLOCKS], U32, align_bytes=64)
-            plane = work.tile([P, UNIT_BLOCKS], U8, align_bytes=64)
+        def quantise(unit, x_sum):
+            codes = work.tile([P, unit[2] * P], U32, align_bytes=64)
+            plane = work.tile([P, unit[2] * P], U8, align_bytes=64)
             nc.vector.quantize_mx(
                 out=codes[:].bitcast(FP8X4),
                 scales=plane[:],
-                in_=x_avg[:].rearrange("p n j -> p (n j)"),
+                in_=x_sum[:].rearrange("p n j -> p (n j)"),
             )
             return codes, plane
 
-        def project_k(codes, plane):
-            kt_banks = []
-            for o in range(OUT_TILES):
-                if o % 2 == 0:
-                    kt_ps = psum_kt.tile([P, 2, UNIT_BLOCKS], F32)
-                    kt_banks.append(kt_ps)
+        def project_direct(unit, codes, plane, banks, t):
+            group = slice(t * P, (t + 1) * P)
+            for which, first, width in unit[3][0]:
+                in_bank = t % (BANK // width)
+                if in_bank == 0:
+                    direct_ps = psum_direct.tile([P, BANK // width, width], F32)
+                    banks.setdefault((which, first, width), []).append(direct_ps)
+                words, w_plane = weights[which]
                 nc.tensor.matmul_mx(
-                    out=kt_ps[:, o % 2, :],
-                    lhsT=wk_words[:, 2 * o * P : 2 * (o + 1) * P].bitcast(FP4X4),
-                    lhsT_scale=wk_plane[:, o * P : (o + 1) * P],
+                    out=banks[(which, first, width)][-1][:, in_bank, :],
+                    lhsT=codes[:, group].bitcast(FP8X4),
+                    lhsT_scale=plane[:, group],
+                    rhs=words[:, 2 * first : 2 * (first + width)].bitcast(FP4X4),
+                    rhs_scale=w_plane[:, first : first + width],
+                    start=True,
+                    stop=True,
+                )
+
+        def finish_direct(unit, banks, outs):
+            groups = unit[2]
+            for which, first, width in unit[3][0]:
+                for k, direct_ps in enumerate(banks[(which, first, width)]):
+                    t0 = k * (BANK // width)
+                    n = min(BANK // width, groups - t0)
+                    nc.vector.scalar_tensor_tensor(
+                        out=outs[which][:, t0 : t0 + n, first : first + width],
+                        in0=direct_ps[:, 0:n, :],
+                        scalar=1.0 / BLOCK_PIXELS,
+                        in1=spread[(which, first, width)][:, 0:n, :],
+                        op0=MULT,
+                        op1=ADD,
+                    )
+                if all(w != which or f <= first for w, f, n in unit[3][0]):
+                    nc.sync.dma_start(out=unit_rows((out_0, out_1)[which], unit), in_=outs[which][:])
+
+        def unit_rows(out, unit):
+            b, first, groups = unit[0:3]
+            rows = out[b, first * P : (first + groups) * P, :]
+            return rows.rearrange("(t m) o -> m t o", t=groups)
+
+        def project(unit, codes, plane, next_unit):
+            groups = unit[2]
+            blocks = groups * P
+            tiles = unit[3][1]
+            turned_sbs = {}
+
+            def project_and_bias(i):
+                which, o = tiles[i]
+                words, w_plane = weights[which]
+                turned_ps = psum_turned.tile([P, blocks], F32)
+                nc.tensor.matmul_mx(
+                    out=turned_ps[:],
+                    lhsT=words[:, 2 * o * P : 2 * (o + 1) * P].bitcast(FP4X4),
+                    lhsT_scale=w_plane[:, o * P : (o + 1) * P],
                     rhs=codes[:].bitcast(FP8X4),
                     rhs_scale=plane[:],
                     start=True,
                     stop=True,
                 )
-            return kt_banks
-
-        def project_q(codes, plane):
-            q_banks = []
-            for t in range(GROUPS):
-                group = slice(t * P, (t + 1) * P)
-                q_ps = psum_q.tile([P, OUT], F32)
-                nc.tensor.matmul_mx(
-                    out=q_ps[:],
-                    lhsT=codes[:, group].bitcast(FP8X4),
-                    lhsT_scale=plane[:, group],
-                    rhs=wq_words[:].bitcast(FP4X4),
-                    rhs_scale=wq_plane[:],
-                    start=True,
-                    stop=True,
-                )
-                q_banks.append(q_ps)
-            return q_banks
-
-        def bias_kt(kt_banks):
-            kt_sb = work.tile([P, OUT_TILES, UNIT_BLOCKS], F32)
-            for o in range(OUT_TILES):
+                turned_sb = turned_pool.tile([P, blocks], F32)
                 nc.scalar.activation(
-                    out=kt_sb[:, o, :],
-                    in_=kt_banks[o // 2][:, o % 2, :],
+                    out=turned_sb[:],
+                    in_=turned_ps[:],
                     func=ACT.Identity,
                     scale=1.0 / BLOCK_PIXELS,
-                    bias=bk_cols[:, o : o + 1],
+                    bias=bias_cols[:, which * OUT_TILES + o : which * OUT_TILES + o + 1],
                 )
-            return kt_sb
+                turned_sbs[i] = turned_sb
 
-        def transpose_k(kt_sb):
-            k_banks = []
-            for t in range(GROUPS):
-                k_ps = psum_k.tile([P, OUT], F32)
-                for o in range(OUT_TILES):
+            q_out = results.tile([P, groups, OUT], F32)
+            k_out = results.tile([P, groups, OUT], F32)
+            outs = (q_out, k_out)
+            banks = {}
+            pool_ps = new_pool_ps(next_unit) if next_unit is not None else None
+            if unit[3][2]:
+                for t in range(groups):
+                    project_direct(unit, codes, plane, banks, t)
+            project_and_bias(0)
+            project_and_bias(1)
+            if not unit[3][2]:
+                for t in range(groups):
+                    project_direct(unit, codes, plane, banks, t)
+            for i in range(len(tiles)):
+                which, o = tiles[i]
+                back_ps = psum_back.tile([P, groups, P], F32)
+                for t in range(groups):
                     nc.tensor.transpose(
-                        k_ps[:, o * P : (o + 1) * P], kt_sb[:, o, t * P : (t + 1) * P], identity[:]
+                        back_ps[:, t, :], turned_sbs[i][:, t * P : (t + 1) * P], identity[:]
                     )
-                k_banks.append(k_ps)
-            return k_banks
+                if next_unit is not None and i < BLOCK_PIXELS:
+                    pool_corner(next_unit, pool_ps, i)
+                nc.scalar.copy(out=outs[which][:, :, o * P : (o + 1) * P], in_=back_ps[:])
+                if all(other != which for other, tile in tiles[i + 1 :]) and all(
+                    w != which for w, first, width in unit[3][0]
+                ):
+                    nc.sync.dma_start(out=unit_rows((out_0, out_1)[which], unit), in_=outs[which][:])
+                if i + 2 < len(tiles):
+                    project_and_bias(i + 2)
+            if next_unit is not None:
+                for corner in range(len(tiles), BLOCK_PIXELS):
+                    pool_corner(next_unit, pool_ps, corner)
+            return banks, outs, pool_ps
 
-        def unit_rows(out, u):
-            first = (u % HALVES) * UNIT_BLOCKS
-            rows = out[u // HALVES, first : first + UNIT_BLOCKS, :]
-            return rows.rearrange("(t m) o -> m t o", t=GROUPS)
-
-        def finish_q(u, q_banks):
-            q_out = results.tile([P, GROUPS, OUT], F32)
-            for t in range(GROUPS):
-                nc.vector.scalar_tensor_tensor(
-                    out=q_out[:, t, :],
-                    in0=q_banks[t][:],
-                    scalar=1.0 / BLOCK_PIXELS,
-                    in1=bq_all[:],
-                    op0=MULT,
-                    op1=ADD,
-                )
-            nc.sync.dma_start(out=unit_rows(out_0, u), in_=q_out[:])
-
-        def finish_k(u, k_banks):
-            k_out = results.tile([P, GROUPS, OUT], F32)
-            for t in range(GROUPS):
-                nc.scalar.copy(out=k_out[:, t, :], in_=k_banks[t][:])
-            nc.sync.dma_start(out=unit_rows(out_1, u), in_=k_out[:])
-
-        pool_ps = pool_on_tensor(0)
-        bq_all, bk_cols = spread_biases()
-        x_avg, q_banks, kt_sb = None, None, None
-        for step in range(UNITS + 2):
-            pooling = step < UNITS
-            projecting = 1 <= step <= UNITS
-            finishing = step >= 2
+        pool_ps = new_pool_ps(units[0])
+        for corner in range(BLOCK_PIXELS):
+            pool_corner(units[0], pool_ps, corner)
+        x_sum_next = round_tensor_sums(units[0], pool_ps)
+        spread, bias_cols = spread_biases()
+        x_sum, projected = None, None
+        for step in range(len(units) + 2):
+            pooling = step < len(units)
+            projecting = 1 <= step <= len(units)
+            next_unit = units[step + 1] if step + 1 < len(units) else None
+            x_sum_before = x_sum
             if pooling:
-                row_sum = add_rows(step)
+                x_sum = x_sum_next if step == 0 else round_tensor_sums(units[step], pool_ps)
+                row_sum = add_rows(units[step])
+            if step >= 2:
+                finish_direct(units[step - 2], projected[0], projected[1])
             if projecting:
-                codes, plane = quantise(x_avg)
-                kt_banks = project_k(codes, plane)
-            if finishing:
-                k_banks = transpose_k(kt_sb)
-                q_banks_to_finish = q_banks
-            if projecting:
-                q_banks = project_q(codes, plane)
+                codes, plane = quantise(units[step - 1], x_sum_before)
             if pooling:
-                x_avg = add_columns(row_sum)
-                round_tensor_sums(pool_ps, x_avg)
-            if step + 1 < UNITS:
-                pool_ps = pool_on_tensor(step + 1)
+                add_columns(units[step], row_sum, x_sum)
             if projecting:
-                kt_sb = bias_kt(kt_banks)
-            if finishing:
-                finish_q(step - 2, q_banks_to_finish)
-                finish_k(step - 2, k_banks)
-            next_image = step // HALVES + IMAGES_AHEAD
-            if step % HALVES == HALVES - 1 and next_image < IMAGES:
-                x_tiles.append(load_image(next_image))
+                projected = project(units[step - 1], codes, plane, next_unit)
+                pool_ps = projected[2]
+            elif next_unit is not None:
+                pool_ps = new_pool_ps(next_unit)
+                for corner in range(BLOCK_PIXELS):
+                    pool_corner(next_unit, pool_ps, corner)
+            if pooling and (next_unit is None or next_unit[0] != units[step][0]):
+                next_image = units[step][0] + IMAGES_AHEAD
+                if next_image < IMAGES:
+                    load_image(next_image)

@@ -29,6 +29,7 @@ BANK = 512
 STEADY = (((0, 0, 256), (0, 256, 128)), ((0, 3), (1, 0), (1, 1), (1, 2), (1, 3)), False)
 MIDDLE = (((0, 0, 512),), ((1, 0), (1, 1), (1, 2), (1, 3)), False)
 DRAIN = (((0, 0, 512), (1, 0, 256)), ((1, 2), (1, 3)), True)
+DIRECT_BEHIND = 2
 LAYOUT = [[(2, STEADY), (2, STEADY)]] + [[(4, STEADY)]] * 5 + [[(2, MIDDLE), (2, MIDDLE)]] + [[(2, DRAIN), (2, DRAIN)]]
 RUN = 4
 PAIR = 2
@@ -54,6 +55,7 @@ def tile_coarseblockattention_pa_t_kernel(
         consts = ctx.enter_context(tc.tile_pool(name="consts", bufs=1))
         images = ctx.enter_context(tc.tile_pool(name="images", bufs=IMAGES_AHEAD))
         work = ctx.enter_context(tc.tile_pool(name="work", bufs=2))
+        sums = ctx.enter_context(tc.tile_pool(name="sums", bufs=1))
         turned_pool = ctx.enter_context(tc.tile_pool(name="turned_pool", bufs=3))
         results = ctx.enter_context(tc.tile_pool(name="results", bufs=4))
         psum_direct = ctx.enter_context(tc.psum_pool(name="psum_direct", bufs=3))
@@ -166,17 +168,42 @@ def tile_coarseblockattention_pa_t_kernel(
             pool_ps = psum_pool.tile([P, PACK, tensor_rows(unit), ROW_BLOCKS], F32)
             return pool_ps
 
-        def add_rows(unit):
+        def gpsimd_rows(index):
+            if index < 3:
+                return 0
+            before = units[index - 3]
+            return 2 * before[2] * sum(width for which, first, width in before[3][0]) // BANK
+
+        def new_row_sum(index):
+            unit = units[index]
+            row_sum = sums.tile([P, PACK, unit[2] * GROUP_ROWS - tensor_rows(unit), WIDTH], F32)
+            return row_sum
+
+        def add_rows_on_gpsimd(index, row_sum):
+            unit = units[index]
+            skipped = tensor_rows(unit)
+            r1 = unit[2] * GROUP_ROWS
+            r0 = r1 - gpsimd_rows(index)
+            rows = unit_pixels(unit)
+            nc.gpsimd.tensor_tensor(
+                out=row_sum[:, :, r0 - skipped : r1 - skipped, :],
+                in0=rows[:, :, r0:r1, 0, :],
+                in1=rows[:, :, r0:r1, 1, :],
+                op=ADD,
+            )
+
+        def add_rows(index, row_sum):
+            unit = units[index]
             b, first, groups = unit[0:3]
             skipped = tensor_rows(unit)
+            last = groups * GROUP_ROWS - gpsimd_rows(index)
             rows = unit_pixels(unit)
-            row_sum = work.tile([P, PACK, groups * GROUP_ROWS - skipped, WIDTH], F32)
             piece_first = 0
             for piece in pieces[b]:
                 low, high = max(piece_first, first), min(piece_first + piece, first + groups)
                 if low < high:
                     r0 = max((low - first) * GROUP_ROWS, skipped)
-                    r1 = (high - first) * GROUP_ROWS
+                    r1 = min((high - first) * GROUP_ROWS, last)
                     nc.vector.tensor_tensor(
                         out=row_sum[:, :, r0 - skipped : r1 - skipped, :],
                         in0=rows[:, :, r0:r1, 0, :],
@@ -184,7 +211,6 @@ def tile_coarseblockattention_pa_t_kernel(
                         op=ADD,
                     )
                 piece_first += piece
-            return row_sum
 
         def round_tensor_sums(unit, pool_ps):
             x_sum = work.tile([P, unit[2] * P, PACK], BF16, align_bytes=64)
@@ -288,12 +314,9 @@ def tile_coarseblockattention_pa_t_kernel(
             outs = (q_out, k_out)
             banks = {}
             pool_ps = new_pool_ps(next_unit) if next_unit is not None else None
-            if unit[3][2]:
-                for t in range(groups):
-                    project_direct(unit, codes, plane, banks, t)
             project_and_bias(0)
             project_and_bias(1)
-            if not unit[3][2]:
+            if unit[3][2]:
                 for t in range(groups):
                     project_direct(unit, codes, plane, banks, t)
             for i in range(len(tiles)):
@@ -312,6 +335,9 @@ def tile_coarseblockattention_pa_t_kernel(
                     nc.sync.dma_start(out=unit_rows((out_0, out_1)[which], unit), in_=outs[which][:])
                 if i + 2 < len(tiles):
                     project_and_bias(i + 2)
+                if i == DIRECT_BEHIND and not unit[3][2]:
+                    for t in range(groups):
+                        project_direct(unit, codes, plane, banks, t)
             if next_unit is not None:
                 for corner in range(len(tiles), BLOCK_PIXELS):
                     pool_corner(next_unit, pool_ps, corner)
@@ -322,7 +348,8 @@ def tile_coarseblockattention_pa_t_kernel(
             pool_corner(units[0], pool_ps, corner)
         x_sum_next = round_tensor_sums(units[0], pool_ps)
         spread, bias_cols = spread_biases()
-        x_sum, projected = None, None
+        x_sum, projected, projected_before = None, None, None
+        row_sum = new_row_sum(0)
         for step in range(len(units) + 2):
             pooling = step < len(units)
             projecting = 1 <= step <= len(units)
@@ -330,13 +357,17 @@ def tile_coarseblockattention_pa_t_kernel(
             x_sum_before = x_sum
             if pooling:
                 x_sum = x_sum_next if step == 0 else round_tensor_sums(units[step], pool_ps)
-                row_sum = add_rows(units[step])
-            if step >= 2:
-                finish_direct(units[step - 2], projected[0], projected[1])
+                add_rows(step, row_sum)
             if projecting:
                 codes, plane = quantise(units[step - 1], x_sum_before)
             if pooling:
                 add_columns(units[step], row_sum, x_sum)
+            if next_unit is not None:
+                row_sum = new_row_sum(step + 1)
+                if gpsimd_rows(step + 1) > 0:
+                    add_rows_on_gpsimd(step + 1, row_sum)
+            if step >= 2:
+                finish_direct(units[step - 2], projected[0], projected[1])
             if projecting:
                 projected = project(units[step - 1], codes, plane, next_unit)
                 pool_ps = projected[2]

@@ -31,7 +31,6 @@ MIDDLE = (((0, 0, 512),), ((1, 0), (1, 1), (1, 2), (1, 3)), False)
 DRAIN = (((0, 0, 512), (1, 0, 256)), ((1, 2), (1, 3)), True)
 DIRECT_BEHIND = 2
 LAYOUT = [[(2, STEADY), (2, STEADY)]] + [[(4, STEADY)]] * 5 + [[(2, MIDDLE), (2, MIDDLE)]] + [[(2, DRAIN), (2, DRAIN)]]
-RUN = 4
 PAIR = 2
 IMAGES_AHEAD = 5
 
@@ -212,20 +211,20 @@ def tile_coarseblockattention_pa_t_kernel(
                     )
                 piece_first += piece
 
+        def pair_words(x_sum):
+            return x_sum[:].rearrange("p (i c) j -> p c j i", i=PAIR)
+
         def round_tensor_sums(unit, pool_ps):
             x_sum = work.tile([P, unit[2] * P, PACK], BF16, align_bytes=64)
-            words = x_sum[:].rearrange("p (c i) j -> p c j i", i=RUN)
             nc.scalar.copy(
-                out=words[:, 0 : tensor_rows(unit) * ROW_BLOCKS // RUN],
-                in_=pool_ps[:].rearrange("p j r c -> p j (r c)").rearrange("p j (c i) -> p c j i", i=RUN),
+                out=pair_words(x_sum)[:, 0 : tensor_rows(unit) * ROW_BLOCKS // PAIR],
+                in_=pool_ps[:].rearrange("p j r c -> p j (r c)").rearrange("p j (c i) -> p c j i", i=PAIR),
             )
             return x_sum
 
         def add_columns(unit, row_sum, x_sum):
             columns = row_sum[:].rearrange("p j r (c i e) -> p (r c) j i e", i=PAIR, e=2)
-            words = x_sum[:, tensor_rows(unit) * ROW_BLOCKS : unit[2] * P, :].rearrange(
-                "p (c i) j -> p c j i", i=PAIR
-            )
+            words = pair_words(x_sum)[:, tensor_rows(unit) * ROW_BLOCKS // PAIR : unit[2] * P // PAIR]
             nc.vector.tensor_tensor(
                 out=words, in0=columns[:, :, :, :, 0], in1=columns[:, :, :, :, 1], op=ADD
             )
@@ -240,8 +239,12 @@ def tile_coarseblockattention_pa_t_kernel(
             )
             return codes, plane
 
+        def slot_columns(unit, t):
+            group = (t % PAIR) * (unit[2] // PAIR) + t // PAIR
+            return slice(group * P, (group + 1) * P)
+
         def project_direct(unit, codes, plane, banks, t):
-            group = slice(t * P, (t + 1) * P)
+            group = slot_columns(unit, t)
             for which, first, width in unit[3][0]:
                 in_bank = t % (BANK // width)
                 if in_bank == 0:
@@ -273,12 +276,17 @@ def tile_coarseblockattention_pa_t_kernel(
                         op1=ADD,
                     )
                 if all(w != which or f <= first for w, f, n in unit[3][0]):
-                    nc.sync.dma_start(out=unit_rows((out_0, out_1)[which], unit), in_=outs[which][:])
+                    store((out_0, out_1)[which], unit, outs[which])
 
         def unit_rows(out, unit):
             b, first, groups = unit[0:3]
             rows = out[b, first * P : (first + groups) * P, :]
-            return rows.rearrange("(t m) o -> m t o", t=groups)
+            return rows.rearrange("(h m i) o -> m h (i o)", h=groups // PAIR, i=PAIR)
+
+        def store(out, unit, result):
+            nc.sync.dma_start(
+                out=unit_rows(out, unit), in_=result[:].rearrange("p (h i) o -> p h (i o)", i=PAIR)
+            )
 
         def project(unit, codes, plane, next_unit):
             groups = unit[2]
@@ -324,7 +332,7 @@ def tile_coarseblockattention_pa_t_kernel(
                 back_ps = psum_back.tile([P, groups, P], F32)
                 for t in range(groups):
                     nc.tensor.transpose(
-                        back_ps[:, t, :], turned_sbs[i][:, t * P : (t + 1) * P], identity[:]
+                        back_ps[:, t, :], turned_sbs[i][:, slot_columns(unit, t)], identity[:]
                     )
                 if next_unit is not None and i < BLOCK_PIXELS:
                     pool_corner(next_unit, pool_ps, i)
@@ -332,7 +340,7 @@ def tile_coarseblockattention_pa_t_kernel(
                 if all(other != which for other, tile in tiles[i + 1 :]) and all(
                     w != which for w, first, width in unit[3][0]
                 ):
-                    nc.sync.dma_start(out=unit_rows((out_0, out_1)[which], unit), in_=outs[which][:])
+                    store((out_0, out_1)[which], unit, outs[which])
                 if i + 2 < len(tiles):
                     project_and_bias(i + 2)
                 if i == DIRECT_BEHIND and not unit[3][2]:

@@ -30,7 +30,7 @@ STEADY = (((0, 0, 256), (0, 256, 128)), ((0, 3), (1, 0), (1, 1), (1, 2), (1, 3))
 MIDDLE = (((0, 0, 512),), ((1, 0), (1, 1), (1, 2), (1, 3)), False)
 DRAIN = (((0, 0, 512), (1, 0, 256)), ((1, 2), (1, 3)), True)
 DIRECT_BEHIND = 2
-LAYOUT = [[(2, STEADY), (2, STEADY)]] + [[(4, STEADY)]] * 5 + [[(2, MIDDLE), (2, MIDDLE)]] + [[(2, DRAIN), (2, DRAIN)]]
+LAYOUT = [[(2, STEADY), (2, STEADY)]] + [[(4, MIDDLE)]] * 5 + [[(2, MIDDLE), (2, MIDDLE)]] + [[(2, DRAIN), (2, DRAIN)]]
 PAIR = 2
 IMAGES_AHEAD = 5
 
@@ -57,10 +57,9 @@ def tile_coarseblockattention_pa_t_kernel(
         sums = ctx.enter_context(tc.tile_pool(name="sums", bufs=1))
         turned_pool = ctx.enter_context(tc.tile_pool(name="turned_pool", bufs=3))
         results = ctx.enter_context(tc.tile_pool(name="results", bufs=4))
-        psum_direct = ctx.enter_context(tc.psum_pool(name="psum_direct", bufs=3))
+        psum_direct = ctx.enter_context(tc.psum_pool(name="psum_direct", bufs=4))
         psum_turned = ctx.enter_context(tc.psum_pool(name="psum_turned", bufs=2))
         psum_back = ctx.enter_context(tc.psum_pool(name="psum_back", bufs=2))
-        psum_pool = ctx.enter_context(tc.psum_pool(name="psum_pool", bufs=1))
 
         def load_piece(x_sb, b, first, groups):
             source = x[b].rearrange("(p j) h w -> p j (h w)", j=PACK)
@@ -163,15 +162,17 @@ def tile_coarseblockattention_pa_t_kernel(
                 stop=(corner == BLOCK_PIXELS - 1),
             )
 
-        def new_pool_ps(unit):
-            pool_ps = psum_pool.tile([P, PACK, tensor_rows(unit), ROW_BLOCKS], F32)
+        def pool_on_tensor(unit):
+            pool_ps = psum_back.tile([P, PACK, tensor_rows(unit), ROW_BLOCKS], F32, name="pool_ps", tag="back_ps")
+            for corner in range(BLOCK_PIXELS):
+                pool_corner(unit, pool_ps, corner)
             return pool_ps
 
         def gpsimd_rows(index):
             if index < 3:
                 return 0
             before = units[index - 3]
-            return 2 * before[2] * sum(width for which, first, width in before[3][0]) // BANK
+            return 3 * before[2] * sum(width for which, first, width in before[3][0]) // (2 * BANK)
 
         def new_row_sum(index):
             unit = units[index]
@@ -214,13 +215,15 @@ def tile_coarseblockattention_pa_t_kernel(
         def pair_words(x_sum):
             return x_sum[:].rearrange("p (i c) j -> p c j i", i=PAIR)
 
-        def round_tensor_sums(unit, pool_ps):
+        def new_x_sum(unit):
             x_sum = work.tile([P, unit[2] * P, PACK], BF16, align_bytes=64)
+            return x_sum
+
+        def round_tensor_sums(unit, pool_ps, x_sum):
             nc.scalar.copy(
                 out=pair_words(x_sum)[:, 0 : tensor_rows(unit) * ROW_BLOCKS // PAIR],
                 in_=pool_ps[:].rearrange("p j r c -> p j (r c)").rearrange("p j (c i) -> p c j i", i=PAIR),
             )
-            return x_sum
 
         def add_columns(unit, row_sum, x_sum):
             columns = row_sum[:].rearrange("p j r (c i e) -> p (r c) j i e", i=PAIR, e=2)
@@ -288,7 +291,7 @@ def tile_coarseblockattention_pa_t_kernel(
                 out=unit_rows(out, unit), in_=result[:].rearrange("p (h i) o -> p h (i o)", i=PAIR)
             )
 
-        def project(unit, codes, plane, next_unit):
+        def project(unit, codes, plane, next_unit, round_sums):
             groups = unit[2]
             blocks = groups * P
             tiles = unit[3][1]
@@ -321,9 +324,10 @@ def tile_coarseblockattention_pa_t_kernel(
             k_out = results.tile([P, groups, OUT], F32)
             outs = (q_out, k_out)
             banks = {}
-            pool_ps = new_pool_ps(next_unit) if next_unit is not None else None
             project_and_bias(0)
             project_and_bias(1)
+            for sums in round_sums:
+                round_tensor_sums(sums[0], sums[1], sums[2])
             if unit[3][2]:
                 for t in range(groups):
                     project_direct(unit, codes, plane, banks, t)
@@ -334,8 +338,6 @@ def tile_coarseblockattention_pa_t_kernel(
                     nc.tensor.transpose(
                         back_ps[:, t, :], turned_sbs[i][:, slot_columns(unit, t)], identity[:]
                     )
-                if next_unit is not None and i < BLOCK_PIXELS:
-                    pool_corner(next_unit, pool_ps, i)
                 nc.scalar.copy(out=outs[which][:, :, o * P : (o + 1) * P], in_=back_ps[:])
                 if all(other != which for other, tile in tiles[i + 1 :]) and all(
                     w != which for w, first, width in unit[3][0]
@@ -346,17 +348,14 @@ def tile_coarseblockattention_pa_t_kernel(
                 if i == DIRECT_BEHIND and not unit[3][2]:
                     for t in range(groups):
                         project_direct(unit, codes, plane, banks, t)
-            if next_unit is not None:
-                for corner in range(len(tiles), BLOCK_PIXELS):
-                    pool_corner(next_unit, pool_ps, corner)
+            pool_ps = pool_on_tensor(next_unit) if next_unit is not None else None
             return banks, outs, pool_ps
 
-        pool_ps = new_pool_ps(units[0])
-        for corner in range(BLOCK_PIXELS):
-            pool_corner(units[0], pool_ps, corner)
-        x_sum_next = round_tensor_sums(units[0], pool_ps)
+        pool_ps = pool_on_tensor(units[0])
+        x_sum = new_x_sum(units[0])
+        round_tensor_sums(units[0], pool_ps, x_sum)
         spread, bias_cols = spread_biases()
-        x_sum, projected, projected_before = None, None, None
+        projected = None
         row_sum = new_row_sum(0)
         for step in range(len(units) + 2):
             pooling = step < len(units)
@@ -364,7 +363,8 @@ def tile_coarseblockattention_pa_t_kernel(
             next_unit = units[step + 1] if step + 1 < len(units) else None
             x_sum_before = x_sum
             if pooling:
-                x_sum = x_sum_next if step == 0 else round_tensor_sums(units[step], pool_ps)
+                if step > 0:
+                    x_sum = new_x_sum(units[step])
                 add_rows(step, row_sum)
             if projecting:
                 codes, plane = quantise(units[step - 1], x_sum_before)
@@ -377,12 +377,11 @@ def tile_coarseblockattention_pa_t_kernel(
             if step >= 2:
                 finish_direct(units[step - 2], projected[0], projected[1])
             if projecting:
-                projected = project(units[step - 1], codes, plane, next_unit)
+                sums_to_round = [(units[step], pool_ps, x_sum)] if pooling else []
+                projected = project(units[step - 1], codes, plane, next_unit, sums_to_round)
                 pool_ps = projected[2]
             elif next_unit is not None:
-                pool_ps = new_pool_ps(next_unit)
-                for corner in range(BLOCK_PIXELS):
-                    pool_corner(next_unit, pool_ps, corner)
+                pool_ps = pool_on_tensor(next_unit)
             if pooling and (next_unit is None or next_unit[0] != units[step][0]):
                 next_image = units[step][0] + IMAGES_AHEAD
                 if next_image < IMAGES:

@@ -28,9 +28,9 @@ IMAGE_GROUPS = PIXELS // GROUP_PIXELS
 BANK = 512
 STEADY = (((0, 0, 256), (0, 256, 128)), ((0, 3), (1, 0), (1, 1), (1, 2), (1, 3)), False)
 MIDDLE = (((0, 0, 512),), ((1, 0), (1, 1), (1, 2), (1, 3)), False)
-DRAIN = (((0, 0, 512), (1, 0, 256)), ((1, 2), (1, 3)), True)
-DIRECT_BEHIND = 2
-LAYOUT = [[(2, STEADY), (2, STEADY)]] + [[(4, MIDDLE)]] * 5 + [[(2, MIDDLE), (2, MIDDLE)]] + [[(2, DRAIN), (2, DRAIN)]]
+DRAIN = (((1, 0, 256), (0, 0, 512)), ((1, 2), (1, 3)), True)
+DIRECT_BEHIND = 1
+LAYOUT = [[(2, STEADY), (2, STEADY)]] + [[(4, MIDDLE)]] * 5 + [[(2, MIDDLE), (2, DRAIN)]] + [[(2, DRAIN), (2, DRAIN)]]
 PAIR = 2
 IMAGES_AHEAD = 5
 
@@ -55,6 +55,7 @@ def tile_coarseblockattention_pa_t_kernel(
         images = ctx.enter_context(tc.tile_pool(name="images", bufs=IMAGES_AHEAD))
         work = ctx.enter_context(tc.tile_pool(name="work", bufs=2))
         sums = ctx.enter_context(tc.tile_pool(name="sums", bufs=1))
+        words_pool = ctx.enter_context(tc.tile_pool(name="words_pool", bufs=4))
         turned_pool = ctx.enter_context(tc.tile_pool(name="turned_pool", bufs=3))
         results = ctx.enter_context(tc.tile_pool(name="results", bufs=4))
         psum_direct = ctx.enter_context(tc.psum_pool(name="psum_direct", bufs=4))
@@ -138,9 +139,9 @@ def tile_coarseblockattention_pa_t_kernel(
                 )
             return words_sb, plane_sb
 
+        load_image(1)
         weights = [load_weight("wq", Wq_words, Wq_scales), load_weight("wk", Wk_words, Wk_scales)]
-
-        for b in range(1, IMAGES_AHEAD):
+        for b in range(2, IMAGES_AHEAD):
             load_image(b)
 
         def tensor_rows(unit):
@@ -216,7 +217,7 @@ def tile_coarseblockattention_pa_t_kernel(
             return x_sum[:].rearrange("p (i c) j -> p c j i", i=PAIR)
 
         def new_x_sum(unit):
-            x_sum = work.tile([P, unit[2] * P, PACK], BF16, align_bytes=64)
+            x_sum = words_pool.tile([P, unit[2] * P, PACK], BF16, align_bytes=64)
             return x_sum
 
         def round_tensor_sums(unit, pool_ps, x_sum):
@@ -278,7 +279,11 @@ def tile_coarseblockattention_pa_t_kernel(
                         op0=MULT,
                         op1=ADD,
                     )
-                if all(w != which or f <= first for w, f, n in unit[3][0]):
+                    if unit == units[-1] and width == OUT:
+                        store_slot((out_0, out_1)[which], unit, outs[which], k)
+                if all(w != which or f <= first for w, f, n in unit[3][0]) and not (
+                    unit == units[-1] and width == OUT
+                ):
                     store((out_0, out_1)[which], unit, outs[which])
 
         def unit_rows(out, unit):
@@ -291,10 +296,19 @@ def tile_coarseblockattention_pa_t_kernel(
                 out=unit_rows(out, unit), in_=result[:].rearrange("p (h i) o -> p h (i o)", i=PAIR)
             )
 
-        def project(unit, codes, plane, next_unit, round_sums):
+        def store_slot(out, unit, result, t):
+            b, first, groups = unit[0:3]
+            rows = out[b, first * P : (first + groups) * P, :]
+            nc.sync.dma_start(
+                out=rows.rearrange("(h m i) o -> m h i o", h=groups // PAIR, i=PAIR)[:, t // PAIR, t % PAIR, :],
+                in_=result[:, t, :],
+            )
+
+        def project(unit, codes, plane, next_unit):
             groups = unit[2]
             blocks = groups * P
             tiles = unit[3][1]
+            early = unit[3][2] or groups < IMAGE_GROUPS
             turned_sbs = {}
 
             def project_and_bias(i):
@@ -326,9 +340,7 @@ def tile_coarseblockattention_pa_t_kernel(
             banks = {}
             project_and_bias(0)
             project_and_bias(1)
-            for sums in round_sums:
-                round_tensor_sums(sums[0], sums[1], sums[2])
-            if unit[3][2]:
+            if early:
                 for t in range(groups):
                     project_direct(unit, codes, plane, banks, t)
             for i in range(len(tiles)):
@@ -345,31 +357,31 @@ def tile_coarseblockattention_pa_t_kernel(
                     store((out_0, out_1)[which], unit, outs[which])
                 if i + 2 < len(tiles):
                     project_and_bias(i + 2)
-                if i == DIRECT_BEHIND and not unit[3][2]:
+                if i == DIRECT_BEHIND and not early:
                     for t in range(groups):
                         project_direct(unit, codes, plane, banks, t)
-            pool_ps = pool_on_tensor(next_unit) if next_unit is not None else None
-            return banks, outs, pool_ps
+            return banks, outs
 
-        pool_ps = pool_on_tensor(units[0])
-        x_sum = new_x_sum(units[0])
-        round_tensor_sums(units[0], pool_ps, x_sum)
+        def pool_and_round(unit):
+            x_sum = new_x_sum(unit)
+            round_tensor_sums(unit, pool_on_tensor(unit), x_sum)
+            return x_sum
+
+        x_sums = [pool_and_round(units[0])]
         spread, bias_cols = spread_biases()
+        x_sums.append(pool_and_round(units[1]))
         projected = None
         row_sum = new_row_sum(0)
         for step in range(len(units) + 2):
             pooling = step < len(units)
             projecting = 1 <= step <= len(units)
             next_unit = units[step + 1] if step + 1 < len(units) else None
-            x_sum_before = x_sum
             if pooling:
-                if step > 0:
-                    x_sum = new_x_sum(units[step])
                 add_rows(step, row_sum)
             if projecting:
-                codes, plane = quantise(units[step - 1], x_sum_before)
+                codes, plane = quantise(units[step - 1], x_sums[step - 1])
             if pooling:
-                add_columns(units[step], row_sum, x_sum)
+                add_columns(units[step], row_sum, x_sums[step])
             if next_unit is not None:
                 row_sum = new_row_sum(step + 1)
                 if gpsimd_rows(step + 1) > 0:
@@ -377,11 +389,9 @@ def tile_coarseblockattention_pa_t_kernel(
             if step >= 2:
                 finish_direct(units[step - 2], projected[0], projected[1])
             if projecting:
-                sums_to_round = [(units[step], pool_ps, x_sum)] if pooling else []
-                projected = project(units[step - 1], codes, plane, next_unit, sums_to_round)
-                pool_ps = projected[2]
-            elif next_unit is not None:
-                pool_ps = pool_on_tensor(next_unit)
+                projected = project(units[step - 1], codes, plane, next_unit)
+            if step + 2 < len(units):
+                x_sums.append(pool_and_round(units[step + 2]))
             if pooling and (next_unit is None or next_unit[0] != units[step][0]):
                 next_image = units[step][0] + IMAGES_AHEAD
                 if next_image < IMAGES:

@@ -47,7 +47,9 @@ def tile_coarseblockattention_pa_t_kernel(
         for groups, plan in LAYOUT[b]:
             units.append((b, first, groups, plan))
             first += groups
-    pieces = [[1, 1, 2], [2, 2]] + [[IMAGE_GROUPS]] * (IMAGES - 2)
+    whole = (0, IMAGE_GROUPS, 0, PACK)
+    pieces = [[(0, 1, 0, PACK), (1, 1, 0, PACK), (2, 2, 0, PACK)]]
+    pieces += [[(0, IMAGE_GROUPS, 0, 2), (0, IMAGE_GROUPS, 2, 2)]] + [[whole]] * (IMAGES - 2)
 
     with ExitStack() as ctx:
         ctx.enter_context(tc.manual_schedule())
@@ -62,23 +64,24 @@ def tile_coarseblockattention_pa_t_kernel(
         psum_turned = ctx.enter_context(tc.psum_pool(name="psum_turned", bufs=2))
         psum_back = ctx.enter_context(tc.psum_pool(name="psum_back", bufs=2))
 
-        def load_piece(x_sb, b, first, groups):
+        def load_piece(x_sb, b, piece):
+            first, groups, j0, n = piece
             source = x[b].rearrange("(p j) h w -> p j (h w)", j=PACK)
             pixels = slice(first * GROUP_PIXELS, (first + groups) * GROUP_PIXELS)
-            nc.sync.dma_start(out=x_sb[:, :, pixels], in_=source[:, :, pixels])
+            nc.sync.dma_start(out=x_sb[:, j0 : j0 + n, pixels], in_=source[:, j0 : j0 + n, pixels])
 
         def load_image(b, first_piece=0):
             if first_piece == 0:
                 x_sb = images.tile([P, PACK, PIXELS], BF16)
                 x_tiles.append(x_sb)
-            for i in range(first_piece, len(pieces[b])):
-                load_piece(x_tiles[b], b, sum(pieces[b][0:i]), pieces[b][i])
+            for piece in pieces[b][first_piece:]:
+                load_piece(x_tiles[b], b, piece)
 
         x_tiles = []
         x_first = images.tile([P, PACK, PIXELS], BF16, name="x_first", tag="x_sb")
         x_tiles.append(x_first)
-        load_piece(x_first, 0, 0, pieces[0][0])
-        load_piece(x_first, 0, pieces[0][0], pieces[0][1])
+        load_piece(x_first, 0, pieces[0][0])
+        load_piece(x_first, 0, pieces[0][1])
 
         bias_row = consts.tile([P, 2, OUT], BF16)
         bias_rows_bf = consts.tile([P, P], BF16)
@@ -199,39 +202,46 @@ def tile_coarseblockattention_pa_t_kernel(
             skipped = tensor_rows(unit)
             last = groups * GROUP_ROWS - gpsimd_rows(index)
             rows = unit_pixels(unit)
-            piece_first = 0
-            for piece in pieces[b]:
-                low, high = max(piece_first, first), min(piece_first + piece, first + groups)
+            for piece_first, piece_groups, j0, n in pieces[b]:
+                low, high = max(piece_first, first), min(piece_first + piece_groups, first + groups)
                 if low < high:
                     r0 = max((low - first) * GROUP_ROWS, skipped)
                     r1 = min((high - first) * GROUP_ROWS, last)
                     nc.vector.tensor_tensor(
-                        out=row_sum[:, :, r0 - skipped : r1 - skipped, :],
-                        in0=rows[:, :, r0:r1, 0, :],
-                        in1=rows[:, :, r0:r1, 1, :],
+                        out=row_sum[:, j0 : j0 + n, r0 - skipped : r1 - skipped, :],
+                        in0=rows[:, j0 : j0 + n, r0:r1, 0, :],
+                        in1=rows[:, j0 : j0 + n, r0:r1, 1, :],
                         op=ADD,
                     )
-                piece_first += piece
 
-        def pair_words(x_sum):
-            return x_sum[:].rearrange("p (i c) j -> p c j i", i=PAIR)
+        def pair_words(unit, x_sum):
+            return x_sum[:].rearrange("p (u i m) j -> p u m j i", u=unit[2] // PAIR, i=PAIR)
+
+        def tensor_words(unit):
+            return tensor_rows(unit) * ROW_BLOCKS // unit[2]
 
         def new_x_sum(unit):
             x_sum = words_pool.tile([P, unit[2] * P, PACK], BF16, align_bytes=64)
             return x_sum
 
         def round_tensor_sums(unit, pool_ps, x_sum):
-            nc.scalar.copy(
-                out=pair_words(x_sum)[:, 0 : tensor_rows(unit) * ROW_BLOCKS // PAIR],
-                in_=pool_ps[:].rearrange("p j r c -> p j (r c)").rearrange("p j (c i) -> p c j i", i=PAIR),
+            sums = pool_ps[:].rearrange("p j r c -> p j (r c)").rearrange(
+                "p j (m u i) -> p u m j i", u=unit[2] // PAIR, i=PAIR
             )
+            for u in range(unit[2] // PAIR):
+                nc.scalar.copy(out=pair_words(unit, x_sum)[:, u, 0 : tensor_words(unit)], in_=sums[:, u])
 
         def add_columns(unit, row_sum, x_sum):
-            columns = row_sum[:].rearrange("p j r (c i e) -> p (r c) j i e", i=PAIR, e=2)
-            words = pair_words(x_sum)[:, tensor_rows(unit) * ROW_BLOCKS // PAIR : unit[2] * P // PAIR]
-            nc.vector.tensor_tensor(
-                out=words, in0=columns[:, :, :, :, 0], in1=columns[:, :, :, :, 1], op=ADD
+            columns = row_sum[:].rearrange("p j r w -> p j (r w)").rearrange(
+                "p j (m u i e) -> p u m j i e", u=unit[2] // PAIR, i=PAIR, e=2
             )
+            for u in range(unit[2] // PAIR):
+                nc.vector.tensor_tensor(
+                    out=pair_words(unit, x_sum)[:, u, tensor_words(unit) : P],
+                    in0=columns[:, u, :, :, :, 0],
+                    in1=columns[:, u, :, :, :, 1],
+                    op=ADD,
+                )
 
         def quantise(unit, x_sum):
             codes = work.tile([P, unit[2] * P], U32, align_bytes=64)
@@ -244,8 +254,7 @@ def tile_coarseblockattention_pa_t_kernel(
             return codes, plane
 
         def slot_columns(unit, t):
-            group = (t % PAIR) * (unit[2] // PAIR) + t // PAIR
-            return slice(group * P, (group + 1) * P)
+            return slice(t * P, (t + 1) * P)
 
         def project_direct(unit, codes, plane, banks, t):
             group = slot_columns(unit, t)
@@ -289,20 +298,16 @@ def tile_coarseblockattention_pa_t_kernel(
         def unit_rows(out, unit):
             b, first, groups = unit[0:3]
             rows = out[b, first * P : (first + groups) * P, :]
-            return rows.rearrange("(h m i) o -> m h (i o)", h=groups // PAIR, i=PAIR)
+            return rows.rearrange("(m t) o -> m t o", t=groups)
 
         def store(out, unit, result):
             nc.sync.dma_start(
-                out=unit_rows(out, unit), in_=result[:].rearrange("p (h i) o -> p h (i o)", i=PAIR)
+                out=unit_rows(out, unit).rearrange("m t o -> m (t o)"),
+                in_=result[:].rearrange("p t o -> p (t o)"),
             )
 
         def store_slot(out, unit, result, t):
-            b, first, groups = unit[0:3]
-            rows = out[b, first * P : (first + groups) * P, :]
-            nc.sync.dma_start(
-                out=rows.rearrange("(h m i) o -> m h i o", h=groups // PAIR, i=PAIR)[:, t // PAIR, t % PAIR, :],
-                in_=result[:, t, :],
-            )
+            nc.sync.dma_start(out=unit_rows(out, unit)[:, t, :], in_=result[:, t, :])
 
         def project(unit, codes, plane, next_unit):
             groups = unit[2]

@@ -70,82 +70,70 @@ def tile_coarseblockattention_pa_t_kernel(
             pixels = slice(first * GROUP_PIXELS, (first + groups) * GROUP_PIXELS)
             nc.sync.dma_start(out=x_sb[:, j0 : j0 + n, pixels], in_=source[:, j0 : j0 + n, pixels])
 
-        def load_image(b, first_piece=0):
-            if first_piece == 0:
-                x_sb = images.tile([P, PACK, PIXELS], BF16)
-                x_tiles.append(x_sb)
-            for piece in pieces[b][first_piece:]:
-                load_piece(x_tiles[b], b, piece)
+        def load_image(b, behind=((), (), ())):
+            x_sb = images.tile([P, PACK, PIXELS], BF16)
+            x_tiles.append(x_sb)
+            for piece, small in zip(pieces[b], behind):
+                load_piece(x_sb, b, piece)
+                for out, in_ in small:
+                    nc.sync.dma_start(out=out, in_=in_)
+
+        bias_rows_bf = consts.tile([P, P], BF16)
+        nc.vector.memset(bias_rows_bf[:], 0.0)
+        bias_dmas = [
+            (bias_rows_bf[which * OUT_TILES : (which + 1) * OUT_TILES, :], bias.rearrange("(o c) -> o c", o=OUT_TILES))
+            for which, bias in enumerate((bq, bk))
+        ]
+
+        weights = []
+        weight_dmas = []
+        for label, words, scales in (("wq", Wq_words, Wq_scales), ("wk", Wk_words, Wk_scales)):
+            words_sb = consts.tile([P, 2 * OUT], U8, align_bytes=64, name=label + "_words")
+            plane_sb = consts.tile([P, OUT], U8, align_bytes=64, name=label + "_plane")
+            nc.vector.memset(plane_sb[:].bitcast(I32), 0)
+            weights.append((words_sb, plane_sb))
+            weight_dmas.append((words_sb[:].bitcast(I32), words[0].bitcast(I32)))
+            for quadrant in range(4):
+                weight_dmas.append(
+                    (
+                        plane_sb[32 * quadrant : 32 * quadrant + 4, :].bitcast(I32),
+                        scales[0, 4 * quadrant : 4 * quadrant + 4, :].bitcast(I32),
+                    )
+                )
 
         x_tiles = []
-        x_first = images.tile([P, PACK, PIXELS], BF16, name="x_first", tag="x_sb")
-        x_tiles.append(x_first)
-        load_piece(x_first, 0, pieces[0][0])
-        load_piece(x_first, 0, pieces[0][1])
+        load_image(0, (bias_dmas, (), weight_dmas[0:3]))
+        load_image(1, (weight_dmas[3:7], weight_dmas[7:10]))
+        for b in range(2, IMAGES_AHEAD):
+            load_image(b)
 
-        bias_row = consts.tile([P, 2, OUT], BF16)
-        bias_rows_bf = consts.tile([P, P], BF16)
-        nc.vector.memset(bias_row[:], 0.0)
-        nc.vector.memset(bias_rows_bf[:], 0.0)
-        for which, bias in enumerate((bq, bk)):
-            nc.sync.dma_start(out=bias_row[0:1, which, :], in_=bias.rearrange("(o c) -> o c", o=1))
-            nc.sync.dma_start(
-                out=bias_rows_bf[which * OUT_TILES : (which + 1) * OUT_TILES, :],
-                in_=bias.rearrange("(o c) -> o c", o=OUT_TILES),
-            )
-        load_image(0, first_piece=2)
-        ones = consts.tile([P, P], BF16)
-        nc.vector.memset(ones[:], 1.0)
         identity = consts.tile([P, P], F32)
         masks.make_identity(nc, identity[:])
         identity_bf = consts.tile([P, P], BF16)
         nc.scalar.copy(out=identity_bf[:], in_=identity[:])
 
         def spread_biases():
-            spread = {}
-            for which in range(2):
-                widest = max(first + width for plan in (STEADY, MIDDLE, DRAIN) for w, first, width in plan[0] if w == which)
-                bias_ps = psum_direct.tile([P, BANK], F32, name="bias_ps", tag="direct_ps")
-                nc.tensor.matmul(
-                    out=bias_ps[:, 0:widest],
-                    lhsT=ones[:],
-                    rhs=bias_row[:, which, 0:widest],
-                    start=True,
-                    stop=True,
-                )
-                for plan in (STEADY, MIDDLE, DRAIN):
-                    for w, first, width in plan[0]:
-                        if w == which and (w, first, width) not in spread:
-                            bias_all = consts.tile(
-                                [P, BANK // width, width], F32, name="bias_all_%d_%d_%d" % (w, first, width)
-                            )
-                            for t in range(BANK // width):
-                                nc.scalar.copy(out=bias_all[:, t, :], in_=bias_ps[:, first : first + width])
-                            spread[(w, first, width)] = bias_all
             bias_rows = consts.tile([P, P], F32)
             nc.scalar.copy(out=bias_rows[:], in_=bias_rows_bf[:])
             cols_ps = psum_back.tile([P, BANK], F32, name="cols_ps", tag="back_ps")
             nc.tensor.transpose(cols_ps[:, 0:P], bias_rows[:], identity[:])
             bias_cols = consts.tile([P, 2 * OUT_TILES], F32)
             nc.scalar.copy(out=bias_cols[:], in_=cols_ps[:, 0 : 2 * OUT_TILES])
+            spread = []
+            for which in range(2):
+                widest = max(first + width for plan in (STEADY, MIDDLE, DRAIN) for w, first, width in plan[0] if w == which)
+                bias_ps = psum_direct.tile([P, BANK], F32, name="bias_ps", tag="direct_ps")
+                for o in range(widest // P):
+                    column = which * OUT_TILES + o
+                    nc.tensor.transpose(
+                        bias_ps[:, o * P : (o + 1) * P],
+                        bias_cols[:, column : column + 1].to_broadcast([P, P]),
+                        identity[:],
+                    )
+                bias_all = consts.tile([P, widest], F32, name="bias_all_%d" % which)
+                nc.scalar.copy(out=bias_all[:], in_=bias_ps[:, 0:widest])
+                spread.append(bias_all)
             return spread, bias_cols
-
-        def load_weight(label, words, scales):
-            words_sb = consts.tile([P, 2 * OUT], U8, align_bytes=64, name=label + "_words")
-            plane_sb = consts.tile([P, OUT], U8, align_bytes=64, name=label + "_plane")
-            nc.vector.memset(plane_sb[:].bitcast(I32), 0)
-            nc.sync.dma_start(out=words_sb[:].bitcast(I32), in_=words[0].bitcast(I32))
-            for quadrant in range(4):
-                nc.sync.dma_start(
-                    out=plane_sb[32 * quadrant : 32 * quadrant + 4, :].bitcast(I32),
-                    in_=scales[0, 4 * quadrant : 4 * quadrant + 4, :].bitcast(I32),
-                )
-            return words_sb, plane_sb
-
-        load_image(1)
-        weights = [load_weight("wq", Wq_words, Wq_scales), load_weight("wk", Wk_words, Wk_scales)]
-        for b in range(2, IMAGES_AHEAD):
-            load_image(b)
 
         def tensor_rows(unit):
             return 3 * unit[2] // 2
@@ -284,7 +272,7 @@ def tile_coarseblockattention_pa_t_kernel(
                         out=outs[which][:, t0 : t0 + n, first : first + width],
                         in0=direct_ps[:, 0:n, :],
                         scalar=1.0 / BLOCK_PIXELS,
-                        in1=spread[(which, first, width)][:, 0:n, :],
+                        in1=spread[which][:, first : first + width].unsqueeze(1).to_broadcast([P, n, width]),
                         op0=MULT,
                         op1=ADD,
                     )

@@ -30,7 +30,7 @@ STEADY = (((0, 0, 256), (0, 256, 128)), ((0, 3), (1, 0), (1, 1), (1, 2), (1, 3))
 MIDDLE = (((0, 0, 512),), ((1, 0), (1, 1), (1, 2), (1, 3)), False)
 DRAIN = (((1, 0, 256), (0, 0, 512)), ((1, 2), (1, 3)), True)
 DIRECT_BEHIND = 1
-LAYOUT = [[(2, STEADY), (2, STEADY)]] + [[(4, MIDDLE)]] * 5 + [[(2, MIDDLE), (2, DRAIN)]] + [[(2, DRAIN), (2, DRAIN)]]
+LAYOUT = [[(4, STEADY)]] + [[(4, MIDDLE)]] * 5 + [[(2, MIDDLE), (2, DRAIN)]] + [[(2, DRAIN), (2, DRAIN)]]
 PAIR = 2
 IMAGES_AHEAD = 5
 
@@ -47,9 +47,7 @@ def tile_coarseblockattention_pa_t_kernel(
         for groups, plan in LAYOUT[b]:
             units.append((b, first, groups, plan))
             first += groups
-    whole = (0, IMAGE_GROUPS, 0, PACK)
-    pieces = [[(0, 1, 0, PACK), (1, 1, 0, PACK), (2, 2, 0, PACK)]]
-    pieces += [[(0, IMAGE_GROUPS, 0, 2), (0, IMAGE_GROUPS, 2, 2)]] + [[whole]] * (IMAGES - 2)
+    pieces = [[(j, 1) for j in range(PACK)], [(0, 2), (2, 2)]] + [[(0, PACK)]] * (IMAGES - 2)
 
     with ExitStack() as ctx:
         ctx.enter_context(tc.manual_schedule())
@@ -65,12 +63,11 @@ def tile_coarseblockattention_pa_t_kernel(
         psum_back = ctx.enter_context(tc.psum_pool(name="psum_back", bufs=2))
 
         def load_piece(x_sb, b, piece):
-            first, groups, j0, n = piece
+            j0, n = piece
             source = x[b].rearrange("(p j) h w -> p j (h w)", j=PACK)
-            pixels = slice(first * GROUP_PIXELS, (first + groups) * GROUP_PIXELS)
-            nc.sync.dma_start(out=x_sb[:, j0 : j0 + n, pixels], in_=source[:, j0 : j0 + n, pixels])
+            nc.sync.dma_start(out=x_sb[:, j0 : j0 + n, :], in_=source[:, j0 : j0 + n, :])
 
-        def load_image(b, behind=((), (), ())):
+        def load_image(b, behind=((), (), (), ())):
             x_sb = images.tile([P, PACK, PIXELS], BF16)
             x_tiles.append(x_sb)
             for piece, small in zip(pieces[b], behind):
@@ -102,7 +99,7 @@ def tile_coarseblockattention_pa_t_kernel(
                 )
 
         x_tiles = []
-        load_image(0, (bias_dmas, (), weight_dmas[0:3]))
+        load_image(0, (bias_dmas, (), (), weight_dmas[0:3]))
         load_image(1, (weight_dmas[3:7], weight_dmas[7:10]))
         for b in range(2, IMAGES_AHEAD):
             load_image(b)
@@ -190,17 +187,13 @@ def tile_coarseblockattention_pa_t_kernel(
             skipped = tensor_rows(unit)
             last = groups * GROUP_ROWS - gpsimd_rows(index)
             rows = unit_pixels(unit)
-            for piece_first, piece_groups, j0, n in pieces[b]:
-                low, high = max(piece_first, first), min(piece_first + piece_groups, first + groups)
-                if low < high:
-                    r0 = max((low - first) * GROUP_ROWS, skipped)
-                    r1 = min((high - first) * GROUP_ROWS, last)
-                    nc.vector.tensor_tensor(
-                        out=row_sum[:, j0 : j0 + n, r0 - skipped : r1 - skipped, :],
-                        in0=rows[:, j0 : j0 + n, r0:r1, 0, :],
-                        in1=rows[:, j0 : j0 + n, r0:r1, 1, :],
-                        op=ADD,
-                    )
+            for j0, n in pieces[b]:
+                nc.vector.tensor_tensor(
+                    out=row_sum[:, j0 : j0 + n, 0 : last - skipped, :],
+                    in0=rows[:, j0 : j0 + n, skipped:last, 0, :],
+                    in1=rows[:, j0 : j0 + n, skipped:last, 1, :],
+                    op=ADD,
+                )
 
         def pair_words(unit, x_sum):
             return x_sum[:].rearrange("p (u i m) j -> p u m j i", u=unit[2] // PAIR, i=PAIR)
@@ -360,9 +353,8 @@ def tile_coarseblockattention_pa_t_kernel(
             round_tensor_sums(unit, pool_on_tensor(unit), x_sum)
             return x_sum
 
-        x_sums = [pool_and_round(units[0])]
         spread, bias_cols = spread_biases()
-        x_sums.append(pool_and_round(units[1]))
+        x_sums = [pool_and_round(units[0]), pool_and_round(units[1])]
         projected = None
         row_sum = new_row_sum(0)
         for step in range(len(units) + 2):
@@ -383,8 +375,9 @@ def tile_coarseblockattention_pa_t_kernel(
                 finish_direct(units[step - 2], projected[0], projected[1])
             if projecting:
                 projected = project(units[step - 1], codes, plane, next_unit)
-            if step + 2 < len(units):
-                x_sums.append(pool_and_round(units[step + 2]))
+            ahead = 1 if step < 2 else 2
+            while len(x_sums) <= min(step + ahead, len(units) - 1):
+                x_sums.append(pool_and_round(units[len(x_sums)]))
             if pooling and (next_unit is None or next_unit[0] != units[step][0]):
                 next_image = units[step][0] + IMAGES_AHEAD
                 if next_image < IMAGES:

@@ -99,8 +99,8 @@ def tile_coarseblockattention_pa_t_kernel(
                 )
 
         x_tiles = []
-        load_image(0, (bias_dmas, (), (), weight_dmas[0:3]))
-        load_image(1, (weight_dmas[3:7], weight_dmas[7:10]))
+        load_image(0, (bias_dmas + weight_dmas[0:1], (), (), weight_dmas[1:5]))
+        load_image(1, ((), weight_dmas[5:10]))
         for b in range(2, IMAGES_AHEAD):
             load_image(b)
 

@@ -33,6 +33,7 @@ DIRECT_BEHIND = 1
 LAYOUT = [[(4, STEADY)]] + [[(4, MIDDLE)]] * 5 + [[(2, MIDDLE), (2, DRAIN)]] + [[(2, DRAIN), (2, DRAIN)]]
 PAIR = 2
 IMAGES_AHEAD = 5
+DMA_ALIGN = 256
 
 FLOPS = 2 * IMAGES * IMAGE_GROUPS * P * CHANNELS * 2 * OUT
 
@@ -68,7 +69,7 @@ def tile_coarseblockattention_pa_t_kernel(
             nc.sync.dma_start(out=x_sb[:, j0 : j0 + n, :], in_=source[:, j0 : j0 + n, :])
 
         def load_image(b, behind=((), (), (), ())):
-            x_sb = images.tile([P, PACK, PIXELS], BF16)
+            x_sb = images.tile([P, PACK, PIXELS], BF16, align_bytes=DMA_ALIGN)
             x_tiles.append(x_sb)
             for piece, small in zip(pieces[b], behind):
                 load_piece(x_sb, b, piece)
@@ -85,7 +86,7 @@ def tile_coarseblockattention_pa_t_kernel(
         weights = []
         weight_dmas = []
         for label, words, scales in (("wq", Wq_words, Wq_scales), ("wk", Wk_words, Wk_scales)):
-            words_sb = consts.tile([P, 2 * OUT], U8, align_bytes=64, name=label + "_words")
+            words_sb = consts.tile([P, 2 * OUT], U8, align_bytes=DMA_ALIGN, name=label + "_words")
             plane_sb = consts.tile([P, OUT], U8, align_bytes=64, name=label + "_plane")
             nc.vector.memset(plane_sb[:].bitcast(I32), 0)
             weights.append((words_sb, plane_sb))
@@ -320,8 +321,8 @@ def tile_coarseblockattention_pa_t_kernel(
                 )
                 turned_sbs[i] = turned_sb
 
-            q_out = results.tile([P, groups, OUT], F32)
-            k_out = results.tile([P, groups, OUT], F32)
+            q_out = results.tile([P, groups, OUT], F32, align_bytes=DMA_ALIGN)
+            k_out = results.tile([P, groups, OUT], F32, align_bytes=DMA_ALIGN)
             outs = (q_out, k_out)
             banks = {}
             project_and_bias(0)

@@ -31,6 +31,7 @@ MIDDLE = (((0, 0, 512),), ((1, 0), (1, 1), (1, 2), (1, 3)), False)
 DRAIN = (((1, 0, 256), (0, 0, 512)), ((1, 2), (1, 3)), True)
 DIRECT_BEHIND = 1
 LAYOUT = [[(4, STEADY)]] + [[(4, MIDDLE)]] * 5 + [[(2, MIDDLE), (2, DRAIN)]] + [[(2, DRAIN), (2, DRAIN)]]
+HEAD_ROWS = {0: 2, 1: 1}
 PAIR = 2
 IMAGES_AHEAD = 5
 DMA_ALIGN = 256
@@ -134,7 +135,7 @@ def tile_coarseblockattention_pa_t_kernel(
             return spread, bias_cols
 
         def tensor_rows(unit):
-            return 3 * unit[2] // 2
+            return 3 * unit[2] // 2 + HEAD_ROWS.get(unit[0], 0)
 
         def unit_pixels(unit):
             b, first, groups = unit[0:3]

@@ -49,7 +49,7 @@ def tile_coarseblockattention_pa_t_kernel(
         for groups, plan in LAYOUT[b]:
             units.append((b, first, groups, plan))
             first += groups
-    pieces = [[(j, 1) for j in range(PACK)], [(0, 2), (2, 2)]] + [[(0, PACK)]] * (IMAGES - 2)
+    pieces = [[(0, 2), (2, 1), (3, 1)], [(0, 2), (2, 2)]] + [[(0, PACK)]] * (IMAGES - 2)
 
     with ExitStack() as ctx:
         ctx.enter_context(tc.manual_schedule())
@@ -101,7 +101,7 @@ def tile_coarseblockattention_pa_t_kernel(
                 )
 
         x_tiles = []
-        load_image(0, (bias_dmas + weight_dmas[0:1], (), (), weight_dmas[1:5]))
+        load_image(0, (bias_dmas + weight_dmas[0:1], (), weight_dmas[1:5]))
         load_image(1, ((), weight_dmas[5:10]))
         for b in range(2, IMAGES_AHEAD):
             load_image(b)
@@ -271,11 +271,7 @@ def tile_coarseblockattention_pa_t_kernel(
                         op0=MULT,
                         op1=ADD,
                     )
-                    if unit == units[-1] and width == OUT:
-                        store_slot((out_0, out_1)[which], unit, outs[which], k)
-                if all(w != which or f <= first for w, f, n in unit[3][0]) and not (
-                    unit == units[-1] and width == OUT
-                ):
+                if all(w != which or f <= first for w, f, n in unit[3][0]):
                     store((out_0, out_1)[which], unit, outs[which])
 
         def unit_rows(out, unit):
@@ -288,9 +284,6 @@ def tile_coarseblockattention_pa_t_kernel(
                 out=unit_rows(out, unit).rearrange("m t o -> m (t o)"),
                 in_=result[:].rearrange("p t o -> p (t o)"),
             )
-
-        def store_slot(out, unit, result, t):
-            nc.sync.dma_start(out=unit_rows(out, unit)[:, t, :], in_=result[:, t, :])
 
         def project(unit, codes, plane, next_unit):
             groups = unit[2]

from contextlib import ExitStack

import concourse.masks as masks
import concourse.mybir as mybir

F32 = mybir.dt.float32
BF16 = mybir.dt.bfloat16
U8 = mybir.dt.uint8
U32 = mybir.dt.uint32
I32 = mybir.dt.int32
FP8X4 = mybir.dt.float8_e4m3fn_x4
FP4X4 = mybir.dt.float4_e2m1fn_x4
ADD = mybir.AluOpType.add
MULT = mybir.AluOpType.mult
ACT = mybir.ActivationFunctionType

P = 128
PACK = 4
IMAGES, CHANNELS, HEIGHT, WIDTH = 8, 512, 64, 32
PIXELS = HEIGHT * WIDTH
BLOCK_PIXELS = 4
OUT = 512
OUT_TILES = OUT // P
ROW_BLOCKS = WIDTH // 2
GROUP_ROWS = P // ROW_BLOCKS
GROUP_PIXELS = P * BLOCK_PIXELS
IMAGE_GROUPS = PIXELS // GROUP_PIXELS
BANK = 512
STEADY = (((0, 0, 256), (0, 256, 128)), ((0, 3), (1, 0), (1, 1), (1, 2), (1, 3)), False)
MIDDLE = (((0, 0, 512),), ((1, 0), (1, 1), (1, 2), (1, 3)), False)
DRAIN = (((1, 0, 256), (0, 0, 512)), ((1, 2), (1, 3)), True)
DIRECT_BEHIND = 1
LAYOUT = [[(4, STEADY)]] + [[(4, MIDDLE)]] * 5 + [[(2, MIDDLE), (2, DRAIN)]] + [[(2, DRAIN), (2, DRAIN)]]
HEAD_ROWS = {0: 2, 1: 1}
PAIR = 2
IMAGES_AHEAD = 5
DMA_ALIGN = 256

FLOPS = 2 * IMAGES * IMAGE_GROUPS * P * CHANNELS * 2 * OUT


def tile_coarseblockattention_pa_t_kernel(
    tc, x, Wq_words, Wq_scales, bq, Wk_words, Wk_scales, bk, out_0, out_1
):
    nc = tc.nc
    units = []
    for b in range(IMAGES):
        first = 0
        for groups, plan in LAYOUT[b]:
            units.append((b, first, groups, plan))
            first += groups
    pieces = [[(0, 2), (2, 1), (3, 1)], [(0, 2), (2, 2)]] + [[(0, PACK)]] * (IMAGES - 2)

    with ExitStack() as ctx:
        ctx.enter_context(tc.manual_schedule())
        consts = ctx.enter_context(tc.tile_pool(name="consts", bufs=1))
        images = ctx.enter_context(tc.tile_pool(name="images", bufs=IMAGES_AHEAD))
        work = ctx.enter_context(tc.tile_pool(name="work", bufs=2))
        sums = ctx.enter_context(tc.tile_pool(name="sums", bufs=1))
        words_pool = ctx.enter_context(tc.tile_pool(name="words_pool", bufs=4))
        turned_pool = ctx.enter_context(tc.tile_pool(name="turned_pool", bufs=3))
        results = ctx.enter_context(tc.tile_pool(name="results", bufs=4))
        psum_direct = ctx.enter_context(tc.psum_pool(name="psum_direct", bufs=4))
        psum_turned = ctx.enter_context(tc.psum_pool(name="psum_turned", bufs=2))
        psum_back = ctx.enter_context(tc.psum_pool(name="psum_back", bufs=2))

        def load_piece(x_sb, b, piece):
            j0, n = piece
            source = x[b].rearrange("(p j) h w -> p j (h w)", j=PACK)
            nc.sync.dma_start(out=x_sb[:, j0 : j0 + n, :], in_=source[:, j0 : j0 + n, :])

        def load_image(b, behind=((), (), (), ())):
            x_sb = images.tile([P, PACK, PIXELS], BF16, align_bytes=DMA_ALIGN)
            x_tiles.append(x_sb)
            for piece, small in zip(pieces[b], behind):
                load_piece(x_sb, b, piece)
                for out, in_ in small:
                    nc.sync.dma_start(out=out, in_=in_)

        bias_rows_bf = consts.tile([P, P], BF16)
        nc.vector.memset(bias_rows_bf[:], 0.0)
        bias_dmas = [
            (bias_rows_bf[which * OUT_TILES : (which + 1) * OUT_TILES, :], bias.rearrange("(o c) -> o c", o=OUT_TILES))
            for which, bias in enumerate((bq, bk))
        ]

        weights = []
        weight_dmas = []
        for label, words, scales in (("wq", Wq_words, Wq_scales), ("wk", Wk_words, Wk_scales)):
            words_sb = consts.tile([P, 2 * OUT], U8, align_bytes=DMA_ALIGN, name=label + "_words")
            plane_sb = consts.tile([P, OUT], U8, align_bytes=64, name=label + "_plane")
            nc.vector.memset(plane_sb[:].bitcast(I32), 0)
            weights.append((words_sb, plane_sb))
            weight_dmas.append((words_sb[:].bitcast(I32), words[0].bitcast(I32)))
            for quadrant in range(4):
                weight_dmas.append(
                    (
                        plane_sb[32 * quadrant : 32 * quadrant + 4, :].bitcast(I32),
                        scales[0, 4 * quadrant : 4 * quadrant + 4, :].bitcast(I32),
                    )
                )

        x_tiles = []
        load_image(0, (bias_dmas + weight_dmas[0:1], (), weight_dmas[1:5]))
        load_image(1, ((), weight_dmas[5:10]))
        for b in range(2, IMAGES_AHEAD):
            load_image(b)

        identity = consts.tile([P, P], F32)
        masks.make_identity(nc, identity[:])
        identity_bf = consts.tile([P, P], BF16)
        nc.scalar.copy(out=identity_bf[:], in_=identity[:])

        def spread_biases():
            bias_rows = consts.tile([P, P], F32)
            nc.scalar.copy(out=bias_rows[:], in_=bias_rows_bf[:])
            cols_ps = psum_back.tile([P, BANK], F32, name="cols_ps", tag="back_ps")
            nc.tensor.transpose(cols_ps[:, 0:P], bias_rows[:], identity[:])
            bias_cols = consts.tile([P, 2 * OUT_TILES], F32)
            nc.scalar.copy(out=bias_cols[:], in_=cols_ps[:, 0 : 2 * OUT_TILES])
            spread = []
            for which in range(2):
                widest = max(first + width for plan in (STEADY, MIDDLE, DRAIN) for w, first, width in plan[0] if w == which)
                bias_ps = psum_direct.tile([P, BANK], F32, name="bias_ps", tag="direct_ps")
                for o in range(widest // P):
                    column = which * OUT_TILES + o
                    nc.tensor.transpose(
                        bias_ps[:, o * P : (o + 1) * P],
                        bias_cols[:, column : column + 1].to_broadcast([P, P]),
                        identity[:],
                    )
                bias_all = consts.tile([P, widest], F32, name="bias_all_%d" % which)
                nc.scalar.copy(out=bias_all[:], in_=bias_ps[:, 0:widest])
                spread.append(bias_all)
            return spread, bias_cols

        def tensor_rows(unit):
            return 3 * unit[2] // 2 + HEAD_ROWS.get(unit[0], 0)

        def unit_pixels(unit):
            b, first, groups = unit[0:3]
            pixels = slice(first * GROUP_PIXELS, (first + groups) * GROUP_PIXELS)
            return x_tiles[b][:, :, pixels].rearrange("p j (r i w) -> p j r i w", i=2, w=WIDTH)

        def pool_corner(unit, pool_ps, corner):
            rows = tensor_rows(unit)
            pixels = unit_pixels(unit).rearrange("p j r i (c e) -> p j r i c e", e=2)
            nc.tensor.matmul(
                out=pool_ps[:, :, 0:rows, :],
                lhsT=identity_bf[:],
                rhs=pixels[:, :, 0:rows, corner // 2, :, corner % 2],
                start=(corner == 0),
                stop=(corner == BLOCK_PIXELS - 1),
            )

        def pool_on_tensor(unit):
            pool_ps = psum_back.tile([P, PACK, tensor_rows(unit), ROW_BLOCKS], F32, name="pool_ps", tag="back_ps")
            for corner in range(BLOCK_PIXELS):
                pool_corner(unit, pool_ps, corner)
            return pool_ps

        def gpsimd_rows(index):
            if index < 3:
                return 0
            before = units[index - 3]
            return 3 * before[2] * sum(width for which, first, width in before[3][0]) // (2 * BANK)

        def new_row_sum(index):
            unit = units[index]
            row_sum = sums.tile([P, PACK, unit[2] * GROUP_ROWS - tensor_rows(unit), WIDTH], F32)
            return row_sum

        def add_rows_on_gpsimd(index, row_sum):
            unit = units[index]
            skipped = tensor_rows(unit)
            r1 = unit[2] * GROUP_ROWS
            r0 = r1 - gpsimd_rows(index)
            rows = unit_pixels(unit)
            nc.gpsimd.tensor_tensor(
                out=row_sum[:, :, r0 - skipped : r1 - skipped, :],
                in0=rows[:, :, r0:r1, 0, :],
                in1=rows[:, :, r0:r1, 1, :],
                op=ADD,
            )

        def add_rows(index, row_sum):
            unit = units[index]
            b, first, groups = unit[0:3]
            skipped = tensor_rows(unit)
            last = groups * GROUP_ROWS - gpsimd_rows(index)
            rows = unit_pixels(unit)
            for j0, n in pieces[b]:
                nc.vector.tensor_tensor(
                    out=row_sum[:, j0 : j0 + n, 0 : last - skipped, :],
                    in0=rows[:, j0 : j0 + n, skipped:last, 0, :],
                    in1=rows[:, j0 : j0 + n, skipped:last, 1, :],
                    op=ADD,
                )

        def pair_words(unit, x_sum):
            return x_sum[:].rearrange("p (u i m) j -> p u m j i", u=unit[2] // PAIR, i=PAIR)

        def tensor_words(unit):
            return tensor_rows(unit) * ROW_BLOCKS // unit[2]

        def new_x_sum(unit):
            x_sum = words_pool.tile([P, unit[2] * P, PACK], BF16, align_bytes=64)
            return x_sum

        def round_tensor_sums(unit, pool_ps, x_sum):
            sums = pool_ps[:].rearrange("p j r c -> p j (r c)").rearrange(
                "p j (m u i) -> p u m j i", u=unit[2] // PAIR, i=PAIR
            )
            for u in range(unit[2] // PAIR):
                nc.scalar.copy(out=pair_words(unit, x_sum)[:, u, 0 : tensor_words(unit)], in_=sums[:, u])

        def add_columns(unit, row_sum, x_sum):
            columns = row_sum[:].rearrange("p j r w -> p j (r w)").rearrange(
                "p j (m u i e) -> p u m j i e", u=unit[2] // PAIR, i=PAIR, e=2
            )
            for u in range(unit[2] // PAIR):
                nc.vector.tensor_tensor(
                    out=pair_words(unit, x_sum)[:, u, tensor_words(unit) : P],
                    in0=columns[:, u, :, :, :, 0],
                    in1=columns[:, u, :, :, :, 1],
                    op=ADD,
                )

        def quantise(unit, x_sum):
            codes = work.tile([P, unit[2] * P], U32, align_bytes=64)
            plane = work.tile([P, unit[2] * P], U8, align_bytes=64)
            nc.vector.quantize_mx(
                out=codes[:].bitcast(FP8X4),
                scales=plane[:],
                in_=x_sum[:].rearrange("p n j -> p (n j)"),
            )
            return codes, plane

        def slot_columns(unit, t):
            return slice(t * P, (t + 1) * P)

        def project_direct(unit, codes, plane, banks, t):
            group = slot_columns(unit, t)
            for which, first, width in unit[3][0]:
                in_bank = t % (BANK // width)
                if in_bank == 0:
                    direct_ps = psum_direct.tile([P, BANK // width, width], F32)
                    banks.setdefault((which, first, width), []).append(direct_ps)
                words, w_plane = weights[which]
                nc.tensor.matmul_mx(
                    out=banks[(which, first, width)][-1][:, in_bank, :],
                    lhsT=codes[:, group].bitcast(FP8X4),
                    lhsT_scale=plane[:, group],
                    rhs=words[:, 2 * first : 2 * (first + width)].bitcast(FP4X4),
                    rhs_scale=w_plane[:, first : first + width],
                    start=True,
                    stop=True,
                )

        def finish_direct(unit, banks, outs):
            groups = unit[2]
            for which, first, width in unit[3][0]:
                for k, direct_ps in enumerate(banks[(which, first, width)]):
                    t0 = k * (BANK // width)
                    n = min(BANK // width, groups - t0)
                    nc.vector.scalar_tensor_tensor(
                        out=outs[which][:, t0 : t0 + n, first : first + width],
                        in0=direct_ps[:, 0:n, :],
                        scalar=1.0 / BLOCK_PIXELS,
                        in1=spread[which][:, first : first + width].unsqueeze(1).to_broadcast([P, n, width]),
                        op0=MULT,
                        op1=ADD,
                    )
                if all(w != which or f <= first for w, f, n in unit[3][0]):
                    store((out_0, out_1)[which], unit, outs[which])

        def unit_rows(out, unit):
            b, first, groups = unit[0:3]
            rows = out[b, first * P : (first + groups) * P, :]
            return rows.rearrange("(m t) o -> m t o", t=groups)

        def store(out, unit, result):
            nc.sync.dma_start(
                out=unit_rows(out, unit).rearrange("m t o -> m (t o)"),
                in_=result[:].rearrange("p t o -> p (t o)"),
            )

        def project(unit, codes, plane, next_unit):
            groups = unit[2]
            blocks = groups * P
            tiles = unit[3][1]
            early = unit[3][2] or groups < IMAGE_GROUPS
            turned_sbs = {}

            def project_and_bias(i):
                which, o = tiles[i]
                words, w_plane = weights[which]
                turned_ps = psum_turned.tile([P, blocks], F32)
                nc.tensor.matmul_mx(
                    out=turned_ps[:],
                    lhsT=words[:, 2 * o * P : 2 * (o + 1) * P].bitcast(FP4X4),
                    lhsT_scale=w_plane[:, o * P : (o + 1) * P],
                    rhs=codes[:].bitcast(FP8X4),
                    rhs_scale=plane[:],
                    start=True,
                    stop=True,
                )
                turned_sb = turned_pool.tile([P, blocks], F32)
                nc.scalar.activation(
                    out=turned_sb[:],
                    in_=turned_ps[:],
                    func=ACT.Identity,
                    scale=1.0 / BLOCK_PIXELS,
                    bias=bias_cols[:, which * OUT_TILES + o : which * OUT_TILES + o + 1],
                )
                turned_sbs[i] = turned_sb

            q_out = results.tile([P, groups, OUT], F32, align_bytes=DMA_ALIGN)
            k_out = results.tile([P, groups, OUT], F32, align_bytes=DMA_ALIGN)
            outs = (q_out, k_out)
            banks = {}
            project_and_bias(0)
            project_and_bias(1)
            if early:
                for t in range(groups):
                    project_direct(unit, codes, plane, banks, t)
            for i in range(len(tiles)):
                which, o = tiles[i]
                back_ps = psum_back.tile([P, groups, P], F32)
                for t in range(groups):
                    nc.tensor.transpose(
                        back_ps[:, t, :], turned_sbs[i][:, slot_columns(unit, t)], identity[:]
                    )
                nc.scalar.copy(out=outs[which][:, :, o * P : (o + 1) * P], in_=back_ps[:])
                if all(other != which for other, tile in tiles[i + 1 :]) and all(
                    w != which for w, first, width in unit[3][0]
                ):
                    store((out_0, out_1)[which], unit, outs[which])
                if i + 2 < len(tiles):
                    project_and_bias(i + 2)
                if i == DIRECT_BEHIND and not early:
                    for t in range(groups):
                        project_direct(unit, codes, plane, banks, t)
            return banks, outs

        def pool_and_round(unit):
            x_sum = new_x_sum(unit)
            round_tensor_sums(unit, pool_on_tensor(unit), x_sum)
            return x_sum

        spread, bias_cols = spread_biases()
        x_sums = [pool_and_round(units[0]), pool_and_round(units[1])]
        projected = None
        row_sum = new_row_sum(0)
        for step in range(len(units) + 2):
            pooling = step < len(units)
            projecting = 1 <= step <= len(units)
            next_unit = units[step + 1] if step + 1 < len(units) else None
            if pooling:
                add_rows(step, row_sum)
            if projecting:
                codes, plane = quantise(units[step - 1], x_sums[step - 1])
            if pooling:
                add_columns(units[step], row_sum, x_sums[step])
            if next_unit is not None:
                row_sum = new_row_sum(step + 1)
                if gpsimd_rows(step + 1) > 0:
                    add_rows_on_gpsimd(step + 1, row_sum)
            if step >= 2:
                finish_direct(units[step - 2], projected[0], projected[1])
            if projecting:
                projected = project(units[step - 1], codes, plane, next_unit)
            ahead = 1 if step < 2 else 2
            while len(x_sums) <= min(step + ahead, len(units) - 1):
                x_sums.append(pool_and_round(units[len(x_sums)]))
            if pooling and (next_unit is None or next_unit[0] != units[step][0]):
                next_image = units[step][0] + IMAGES_AHEAD
                if next_image < IMAGES:
                    load_image(next_image)
